import numpy as np
import ml_dtypes


def mxq(x, axis, fmt="e4m3"):
    dtype, down = {"e4m3": (ml_dtypes.float8_e4m3fn, 7), "e5m2": (ml_dtypes.float8_e5m2, 14)}[fmt]
    v = np.moveaxis(np.asarray(x, np.float32).astype(ml_dtypes.bfloat16).astype(np.float64), axis, -1)
    blocks = v.reshape(v.shape[:-1] + (-1, 32))
    amax = np.abs(blocks).max(-1, keepdims=True)
    byte = np.maximum(np.where(amax > 0, np.frexp(amax)[1] - 1 + 127, 0) - down, 1)
    scale = np.exp2(byte - 127.0)
    codes = (blocks / scale).astype(np.float32).astype(dtype).astype(np.float64)
    return np.moveaxis((codes * scale).reshape(v.shape), -1, axis)


WIDE = False


def mx_kscale(k):
    if not WIDE:
        return np.ones(k)
    levels = np.array([20, 0, 10, 5, 0])
    a = np.random.permutation(np.resize(levels, k // 512 * 4)).reshape(k // 512, 4)
    idx = np.arange(k)
    return np.exp2(a[idx // 512, idx % 128 // 32])


BF16 = ml_dtypes.bfloat16


def bf(x):
    return np.asarray(x, np.float32).astype(BF16)


def f64(x):
    return np.asarray(x).astype(np.float64)


B, IN, OUT, ND, R = 1024, 1024, 256, 8, 4
GS = 16.0


def kernel_probs(x, c):
    x2 = np.sum(x * x, axis=-1, keepdims=True)
    c2 = np.sum(c * c, axis=-1)[None, :]
    d2 = x2 - 2.0 * (x @ c.T) + c2
    return np.exp(-d2 / 2.0)


def setup_inputs():
    s = mx_kscale(B)[:, None]
    p = np.random.standard_normal((R, IN)) / np.sqrt(IN)
    a = np.sqrt(2.0 / R)
    x0 = bf(np.random.standard_normal((B, R)) @ p * a)
    centers = bf((np.random.standard_normal((OUT * ND, R)) @ p * a).reshape(OUT, ND, IN))
    g = bf(np.random.standard_normal((B, OUT)) * np.exp2(np.random.randint(-12, 1, (B, 1))) * GS / s)
    probs = kernel_probs(f64(x0), f64(centers).reshape(OUT * ND, IN))
    return {"x": bf(f64(x0) * s), "centers": centers, "probs": np.asarray(probs, np.float32), "grad_out": g}


def reference(x, centers, probs, grad_out):
    x = f64(x)
    c = f64(centers).reshape(OUT * ND, IN)
    pr = f64(probs).reshape(B, OUT, ND)
    hot = np.where(pr == np.max(pr, axis=-1, keepdims=True), 1.0, 0.0)
    hot = hot / np.sum(hot, axis=-1, keepdims=True)
    e = (f64(grad_out)[:, :, None] * (((ND + 1) * hot - 1.0) / ND) * pr).reshape(B, OUT * ND)
    r = np.sum(e, axis=0)
    gc = (mxq(e, 0, "e5m2").T @ mxq(x, 0, "e4m3")) - c * r[:, None]
    return gc.reshape(OUT, ND, IN)

@@ -1,0 +1,284 @@
+import concourse.mybir as mybir
+
+F32 = mybir.dt.float32
+BF16 = mybir.dt.bfloat16
+U32 = mybir.dt.uint32
+U8 = mybir.dt.uint8
+E4M3_X4 = mybir.dt.float8_e4m3fn_x4
+E5M2_X4 = mybir.dt.float8_e5m2_x4
+ALU = mybir.AluOpType
+ACT = mybir.ActivationFunctionType
+AXIS = mybir.AxisListType
+
+TOKENS, IN, OUT, ND = 1024, 1024, 256, 8
+ROWS = OUT * ND
+P = 128
+PACK = 4
+K_PASS = P * PACK
+PASSES = TOKENS // K_PASS
+SLICES = PASSES * PACK
+M_TILE = 128
+N_TILE = 512
+CHUNK = 256
+CHUNKS = ROWS // CHUNK
+CHUNK_OUT = CHUNK // ND
+GROUPS = SLICES * CHUNK_OUT
+HALVES = 2
+ROUNDS = CHUNKS // HALVES
+CHUNK_TILES = CHUNK // M_TILE
+RUN = 4
+
+FLOPS = 2 * TOKENS * ROWS * IN
+
+
+def regroup(nc, grouped, rows):
+    nc.scalar.copy(
+        out=grouped.rearrange("p (a i) t -> p a t i", i=RUN),
+        in_=rows.rearrange("p t (a i) -> p a t i", i=RUN),
+    )
+
+
+def over_group(field):
+    return field.unsqueeze(2).to_broadcast([P, GROUPS, ND])
+
+
+def groups_of(tile_ap):
+    return tile_ap.rearrange("p c t (o d) -> p (c t o) d", d=ND)
+
+
+def tile_pnn_v_kernel(tc, x, centers, probs, grad_out, out):
+    nc = tc.nc
+    centers_rows = centers.rearrange("o d i -> (o d) i")
+    out_rows = out.rearrange("o d i -> (o d) i")
+
+    with tc.tile_pool(name="keep", bufs=1) as keep, tc.tile_pool(name="work", bufs=HALVES) as work, tc.tile_pool(
+        name="next_round", bufs=2 * HALVES
+    ) as next_round, tc.psum_pool(name="acc_pool", bufs=6) as acc_pool, tc.psum_pool(
+        name="sum_pool", bufs=1
+    ) as sum_pool, tc.manual_schedule():
+        probs_sb = []
+        centers_sb = []
+        g_raw = keep.tile([P, PASSES, PACK, OUT], BF16)
+        x_raw = keep.tile([P, PASSES, PACK, IN], BF16)
+        for k in range(CHUNKS):
+            cols = slice(k * CHUNK, (k + 1) * CHUNK)
+            pr = keep.tile([P, PASSES, PACK, CHUNK], F32, name="probs%d" % k)
+            for c in range(PASSES):
+                tokens = slice(c * K_PASS, (c + 1) * K_PASS)
+                nc.sync.dma_start(out=pr[:, c], in_=probs[tokens, cols].rearrange("(p t) j -> p t j", t=PACK))
+            probs_sb.append(pr)
+            if k == HALVES - 1:
+                for c in range(PASSES):
+                    tokens = slice(c * K_PASS, (c + 1) * K_PASS)
+                    nc.sync.dma_start(out=g_raw[:, c], in_=grad_out[tokens, :].rearrange("(p t) o -> p t o", t=PACK))
+                for c in range(PASSES):
+                    tokens = slice(c * K_PASS, (c + 1) * K_PASS)
+                    nc.sync.dma_start(out=x_raw[:, c], in_=x[tokens, :].rearrange("(p t) i -> p t i", t=PACK))
+            cen = keep.tile([P, CHUNK_TILES, IN], BF16, name="centers%d" % k)
+            nc.sync.dma_start(out=cen[:], in_=centers_rows[cols, :].rearrange("(a p) i -> p a i", p=P))
+            centers_sb.append(cen)
+
+        ones = keep.tile([P, 1], F32)
+        nc.vector.memset(ones[:], 1.0)
+        x_codes = keep.tile([P, PASSES, IN], U32, align_bytes=64)
+        x_scales = keep.tile([P, PASSES, IN], U8, align_bytes=64)
+
+        def field(name):
+            return work.tile([P, GROUPS], F32, name=name)
+
+        def both(step, chunks):
+            return [step(chunk) for chunk in chunks]
+
+        def scale_g(ch):
+            g_chunk = g_raw[:].rearrange("p c t o -> p (c t) o")[:, :, ch["k"] * CHUNK_OUT : (ch["k"] + 1) * CHUNK_OUT]
+            ch["u"] = field("u")
+            nc.scalar.mul(out=ch["u"][:].rearrange("p (s o) -> p s o", s=SLICES), in_=g_chunk, mul=-0.125)
+            ch["g9"] = field("g9")
+            nc.scalar.mul(out=ch["g9"][:].rearrange("p (s o) -> p s o", s=SLICES), in_=g_chunk, mul=-1.125)
+
+        def find_top(ch):
+            ch["top"] = field("top")
+            nc.vector.tensor_reduce(out=ch["top"][:], in_=groups_of(ch["e"][:]), axis=AXIS.X, op=ALU.max)
+
+        def mark_top(ch):
+            ch["is_top"] = work.tile([P, GROUPS, ND], BF16, name="is_top")
+            nc.vector.tensor_tensor(
+                out=ch["is_top"][:], in0=groups_of(ch["e"][:]), in1=over_group(ch["top"][:]), op=ALU.is_equal
+            )
+
+        def count_8_to_4(ch):
+            ch["n4"] = work.tile([P, GROUPS, 4], BF16, name="n4")
+            nc.vector.tensor_tensor(
+                out=ch["n4"][:], in0=ch["is_top"][:, :, 0:4], in1=ch["is_top"][:, :, 4:8], op=ALU.add
+            )
+
+        def count_4_to_2(ch):
+            ch["n2"] = work.tile([P, GROUPS, 2], BF16, name="n2")
+            nc.vector.tensor_tensor(out=ch["n2"][:], in0=ch["n4"][:, :, 0:2], in1=ch["n4"][:, :, 2:4], op=ALU.add)
+
+        def count_2_to_1(ch):
+            ch["n"] = field("n")
+            nc.vector.tensor_tensor(
+                out=ch["n"][:].unsqueeze(2), in0=ch["n2"][:, :, 0:1], in1=ch["n2"][:, :, 1:2], op=ALU.add
+            )
+
+        def guess_inverse(ch):
+            nn = field("nn")
+            nc.scalar.activation(out=nn[:], in_=ch["n"][:], func=ACT.Square)
+            ch["guess"] = field("guess")
+            nc.scalar.activation(out=ch["guess"][:], in_=nn[:], func=ACT.Abs_reciprocal_sqrt)
+
+        def scale_probs(ch):
+            nc.vector.tensor_tensor(
+                out=groups_of(ch["e"][:]), in0=groups_of(ch["e"][:]), in1=over_group(ch["u"][:]), op=ALU.mult
+            )
+
+        def g9_times_top(ch):
+            ch["g9_top"] = field("g9_top")
+            nc.vector.tensor_tensor(out=ch["g9_top"][:], in0=ch["g9"][:], in1=ch["top"][:], op=ALU.mult)
+
+        def newton_1(ch):
+            ch["ng"] = field("ng")
+            nc.vector.tensor_tensor(out=ch["ng"][:], in0=ch["n"][:], in1=ch["guess"][:], op=ALU.mult)
+
+        def newton_2(ch):
+            ch["neg_inv_n"] = field("neg_inv_n")
+            nc.vector.scalar_tensor_tensor(
+                out=ch["neg_inv_n"][:], in0=ch["ng"][:], scalar=2.0, in1=ch["guess"][:], op0=ALU.subtract, op1=ALU.mult
+            )
+
+        def share_bonus(ch):
+            ch["bonus"] = field("bonus")
+            nc.vector.tensor_tensor(out=ch["bonus"][:], in0=ch["g9_top"][:], in1=ch["neg_inv_n"][:], op=ALU.mult)
+
+        def place_bonus(ch):
+            ch["extra"] = work.tile([P, GROUPS, ND], F32, name="extra")
+            nc.vector.tensor_tensor(
+                out=ch["extra"][:], in0=ch["is_top"][:], in1=over_group(ch["bonus"][:]), op=ALU.mult
+            )
+
+        def add_bonus(ch):
+            nc.vector.tensor_tensor(out=groups_of(ch["e"][:]), in0=groups_of(ch["e"][:]), in1=ch["extra"][:], op=ALU.add)
+
+        def round_e(ch):
+            ch["e_grouped"] = next_round.tile([P, PASSES, CHUNK, PACK], BF16, align_bytes=64, name="e_grouped")
+            for c in range(PASSES):
+                regroup(nc, ch["e_grouped"][:, c], ch["e"][:, c])
+
+        def quantise_e(ch):
+            ch["codes"] = next_round.tile([P, PASSES, CHUNK], U32, align_bytes=64, name="e_codes")
+            ch["scales"] = next_round.tile([P, PASSES, CHUNK], U8, align_bytes=64, name="e_scales")
+            nc.vector.quantize_mx(
+                out=ch["codes"][:].rearrange("p c j -> p (c j)").bitcast(E5M2_X4),
+                scales=ch["scales"][:].rearrange("p c j -> p (c j)"),
+                in_=ch["e_grouped"][:].rearrange("p c j t -> p (c j t)"),
+            )
+
+        def regroup_x():
+            grouped = []
+            for c in range(PASSES):
+                x_grouped = keep.tile([P, IN, PACK], BF16, align_bytes=64, name="x_grouped%d" % c)
+                regroup(nc, x_grouped[:], x_raw[:, c])
+                grouped.append(x_grouped)
+            return grouped
+
+        def quantise_x(grouped):
+            for c in range(PASSES):
+                nc.vector.quantize_mx(
+                    out=x_codes[:, c].bitcast(E4M3_X4),
+                    scales=x_scales[:, c],
+                    in_=grouped[c][:].rearrange("p i t -> p (i t)"),
+                )
+
+        def sum_tokens(chunks):
+            r_sum = sum_pool.tile([P, HALVES * CHUNK_TILES], F32)
+            for ch in chunks:
+                for a in range(CHUNK_TILES):
+                    col = (ch["k"] % HALVES) * CHUNK_TILES + a
+                    for s in range(SLICES):
+                        nc.tensor.matmul(
+                            out=r_sum[:, col : col + 1],
+                            lhsT=ch["e"][:, s // PACK, s % PACK, a * M_TILE : (a + 1) * M_TILE],
+                            rhs=ones[:],
+                            start=(s == 0),
+                            stop=(s == SLICES - 1),
+                        )
+            neg_r = next_round.tile([P, HALVES * CHUNK_TILES], F32)
+            nc.scalar.mul(out=neg_r[:], in_=r_sum[:], mul=-1.0)
+            return neg_r
+
+        def multiply(ch):
+            ch["acc"] = []
+            for a in range(CHUNK_TILES):
+                rows = slice(a * M_TILE, (a + 1) * M_TILE)
+                for h in range(IN // N_TILE):
+                    n_cols = slice(h * N_TILE, (h + 1) * N_TILE)
+                    acc = acc_pool.tile([P, N_TILE], F32)
+                    for c in range(PASSES):
+                        nc.tensor.matmul_mx(
+                            out=acc[:],
+                            lhsT=ch["codes"][:, c, rows].bitcast(E5M2_X4),
+                            lhsT_scale=ch["scales"][:, c, rows],
+                            rhs=x_codes[:, c, n_cols].bitcast(E4M3_X4),
+                            rhs_scale=x_scales[:, c, n_cols],
+                            start=(c == 0),
+                            stop=(c == PASSES - 1),
+                        )
+                    ch["acc"].append((a, n_cols, acc))
+
+        def finish(ch, neg_r):
+            results = [next_round.tile([P, IN], F32, name="result") for a in range(CHUNK_TILES)]
+            for a, n_cols, acc in ch["acc"]:
+                col = (ch["k"] % HALVES) * CHUNK_TILES + a
+                nc.vector.scalar_tensor_tensor(
+                    out=results[a][:, n_cols],
+                    in0=centers_sb[ch["k"]][:, a, n_cols],
+                    scalar=neg_r[:, col : col + 1],
+                    in1=acc[:],
+                    op0=ALU.mult,
+                    op1=ALU.add,
+                )
+            for a in range(CHUNK_TILES):
+                first = ch["k"] * CHUNK + a * M_TILE
+                nc.sync.dma_start(out=out_rows[first : first + M_TILE, :], in_=results[a][:])
+
+        def chunks_of(rnd):
+            return [{"k": rnd * HALVES + i, "e": probs_sb[rnd * HALVES + i]} for i in range(HALVES)]
+
+        last = []
+        now = chunks_of(0)
+        both(scale_g, now)
+        both(find_top, now)
+        for rnd in range(ROUNDS + 1):
+            after = chunks_of(rnd + 1) if rnd + 1 < ROUNDS else []
+            both(mark_top, now)
+            both(count_8_to_4, now)
+            both(count_4_to_2, now)
+            both(count_2_to_1, now)
+            both(guess_inverse, now)
+            if rnd == 0:
+                x_grouped = regroup_x()
+            if rnd == 1:
+                quantise_x(x_grouped)
+            both(quantise_e, last)
+            if last:
+                multiply(last[0])
+            both(scale_probs, now)
+            both(g9_times_top, now)
+            both(newton_1, now)
+            both(newton_2, now)
+            both(share_bonus, now)
+            both(place_bonus, now)
+            both(add_bonus, now)
+            both(round_e, now)
+            both(scale_g, after)
+            if last:
+                finish(last[0], neg_r)
+                multiply(last[1])
+            both(find_top, after)
+            if last:
+                finish(last[1], neg_r)
+            if now:
+                neg_r = sum_tokens(now)
+            last = now
+            now = after

@@ -158,7 +158,7 @@ def tile_pnn_v_kernel(tc, x, centers, probs, grad_out, out):
             )
 
         def add_bonus(ch):
-            nc.vector.tensor_tensor(out=groups_of(ch["e"][:]), in0=groups_of(ch["e"][:]), in1=ch["extra"][:], op=ALU.add)
+            nc.gpsimd.tensor_tensor(out=groups_of(ch["e"][:]), in0=groups_of(ch["e"][:]), in1=ch["extra"][:], op=ALU.add)
 
         def round_e(ch):
             ch["e_grouped"] = next_round.tile([P, PASSES, CHUNK, PACK], BF16, align_bytes=64, name="e_grouped")

@@ -26,6 +26,7 @@ GROUPS = SLICES * CHUNK_OUT
 HALVES = 2
 ROUNDS = CHUNKS // HALVES
 CHUNK_TILES = CHUNK // M_TILE
+ONES = 64
 RUN = 4
 
 FLOPS = 2 * TOKENS * ROWS * IN
@@ -53,7 +54,7 @@ def tile_pnn_v_kernel(tc, x, centers, probs, grad_out, out):
 
     with tc.tile_pool(name="keep", bufs=1) as keep, tc.tile_pool(name="work", bufs=HALVES) as work, tc.tile_pool(
         name="next_round", bufs=2 * HALVES
-    ) as next_round, tc.psum_pool(name="acc_pool", bufs=6) as acc_pool, tc.psum_pool(
+    ) as next_round, tc.psum_pool(name="acc_pool", bufs=7) as acc_pool, tc.psum_pool(
         name="sum_pool", bufs=1
     ) as sum_pool, tc.manual_schedule():
         probs_sb = []
@@ -78,7 +79,7 @@ def tile_pnn_v_kernel(tc, x, centers, probs, grad_out, out):
             nc.sync.dma_start(out=cen[:], in_=centers_rows[cols, :].rearrange("(a p) i -> p a i", p=P))
             centers_sb.append(cen)
 
-        ones = keep.tile([P, 1], F32)
+        ones = keep.tile([P, ONES], F32)
         nc.vector.memset(ones[:], 1.0)
         x_codes = keep.tile([P, PASSES, IN], U32, align_bytes=64)
         x_scales = keep.tile([P, PASSES, IN], U8, align_bytes=64)
@@ -93,11 +94,9 @@ def tile_pnn_v_kernel(tc, x, centers, probs, grad_out, out):
             g_chunk = g_raw[:].rearrange("p c t o -> p (c t) o")[:, :, ch["k"] * CHUNK_OUT : (ch["k"] + 1) * CHUNK_OUT]
             ch["u"] = field("u")
             nc.scalar.mul(out=ch["u"][:].rearrange("p (s o) -> p s o", s=SLICES), in_=g_chunk, mul=-0.125)
-            ch["g9"] = field("g9")
-            nc.scalar.mul(out=ch["g9"][:].rearrange("p (s o) -> p s o", s=SLICES), in_=g_chunk, mul=-1.125)
 
         def find_top(ch):
-            ch["top"] = field("top")
+            ch["top"] = next_round.tile([P, GROUPS], F32, name="top")
             nc.vector.tensor_reduce(out=ch["top"][:], in_=groups_of(ch["e"][:]), axis=AXIS.X, op=ALU.max)
 
         def mark_top(ch):
@@ -128,15 +127,6 @@ def tile_pnn_v_kernel(tc, x, centers, probs, grad_out, out):
             ch["guess"] = field("guess")
             nc.scalar.activation(out=ch["guess"][:], in_=nn[:], func=ACT.Abs_reciprocal_sqrt)
 
-        def scale_probs(ch):
-            nc.vector.tensor_tensor(
-                out=groups_of(ch["e"][:]), in0=groups_of(ch["e"][:]), in1=over_group(ch["u"][:]), op=ALU.mult
-            )
-
-        def g9_times_top(ch):
-            ch["g9_top"] = field("g9_top")
-            nc.vector.tensor_tensor(out=ch["g9_top"][:], in0=ch["g9"][:], in1=ch["top"][:], op=ALU.mult)
-
         def newton_1(ch):
             ch["ng"] = field("ng")
             nc.vector.tensor_tensor(out=ch["ng"][:], in0=ch["n"][:], in1=ch["guess"][:], op=ALU.mult)
@@ -147,18 +137,25 @@ def tile_pnn_v_kernel(tc, x, centers, probs, grad_out, out):
                 out=ch["neg_inv_n"][:], in0=ch["ng"][:], scalar=2.0, in1=ch["guess"][:], op0=ALU.subtract, op1=ALU.mult
             )
 
-        def share_bonus(ch):
-            ch["bonus"] = field("bonus")
-            nc.vector.tensor_tensor(out=ch["bonus"][:], in0=ch["g9_top"][:], in1=ch["neg_inv_n"][:], op=ALU.mult)
-
-        def place_bonus(ch):
-            ch["extra"] = work.tile([P, GROUPS, ND], F32, name="extra")
-            nc.vector.tensor_tensor(
-                out=ch["extra"][:], in0=ch["is_top"][:], in1=over_group(ch["bonus"][:]), op=ALU.mult
+        def share_top(ch):
+            ch["share"] = field("share")
+            nc.vector.scalar_tensor_tensor(
+                out=ch["share"][:], in0=ch["neg_inv_n"][:], scalar=9.0, in1=ch["top"][:], op0=ALU.mult, op1=ALU.mult
             )
 
-        def add_bonus(ch):
-            nc.gpsimd.tensor_tensor(out=groups_of(ch["e"][:]), in0=groups_of(ch["e"][:]), in1=ch["extra"][:], op=ALU.add)
+        def place_share(ch):
+            ch["extra"] = work.tile([P, GROUPS, ND], F32, name="extra")
+            nc.vector.tensor_tensor(
+                out=ch["extra"][:], in0=ch["is_top"][:], in1=over_group(ch["share"][:]), op=ALU.mult
+            )
+
+        def add_share(ch):
+            nc.vector.tensor_tensor(out=groups_of(ch["e"][:]), in0=groups_of(ch["e"][:]), in1=ch["extra"][:], op=ALU.add)
+
+        def times_g(ch):
+            nc.vector.tensor_tensor(
+                out=groups_of(ch["e"][:]), in0=groups_of(ch["e"][:]), in1=over_group(ch["u"][:]), op=ALU.mult
+            )
 
         def round_e(ch):
             ch["e_grouped"] = next_round.tile([P, PASSES, CHUNK, PACK], BF16, align_bytes=64, name="e_grouped")
@@ -191,20 +188,20 @@ def tile_pnn_v_kernel(tc, x, centers, probs, grad_out, out):
                 )
 
         def sum_tokens(chunks):
-            r_sum = sum_pool.tile([P, HALVES * CHUNK_TILES], F32)
+            r_sum = sum_pool.tile([P, HALVES * CHUNK_TILES, ONES], F32)
             for ch in chunks:
                 for a in range(CHUNK_TILES):
                     col = (ch["k"] % HALVES) * CHUNK_TILES + a
                     for s in range(SLICES):
                         nc.tensor.matmul(
-                            out=r_sum[:, col : col + 1],
+                            out=r_sum[:, col, :],
                             lhsT=ch["e"][:, s // PACK, s % PACK, a * M_TILE : (a + 1) * M_TILE],
                             rhs=ones[:],
                             start=(s == 0),
                             stop=(s == SLICES - 1),
                         )
             neg_r = next_round.tile([P, HALVES * CHUNK_TILES], F32)
-            nc.scalar.mul(out=neg_r[:], in_=r_sum[:], mul=-1.0)
+            nc.scalar.mul(out=neg_r[:], in_=r_sum[:, :, 0], mul=-1.0)
             return neg_r
 
         def multiply(ch):
@@ -263,22 +260,21 @@ def tile_pnn_v_kernel(tc, x, centers, probs, grad_out, out):
             both(quantise_e, last)
             if last:
                 multiply(last[0])
-            both(scale_probs, now)
-            both(g9_times_top, now)
+            both(find_top, after)
             both(newton_1, now)
             both(newton_2, now)
-            both(share_bonus, now)
-            both(place_bonus, now)
-            both(add_bonus, now)
-            both(round_e, now)
-            both(scale_g, after)
+            both(share_top, now)
+            both(place_share, now)
             if last:
                 finish(last[0], neg_r)
                 multiply(last[1])
-            both(find_top, after)
+            both(add_share, now)
+            both(times_g, now)
+            both(round_e, now)
             if last:
                 finish(last[1], neg_r)
             if now:
                 neg_r = sum_tokens(now)
+            both(scale_g, after)
             last = now
             now = after

@@ -90,11 +90,6 @@ def tile_pnn_v_kernel(tc, x, centers, probs, grad_out, out):
         def both(step, chunks):
             return [step(chunk) for chunk in chunks]
 
-        def scale_g(ch):
-            g_chunk = g_raw[:].rearrange("p c t o -> p (c t) o")[:, :, ch["k"] * CHUNK_OUT : (ch["k"] + 1) * CHUNK_OUT]
-            ch["u"] = field("u")
-            nc.scalar.mul(out=ch["u"][:].rearrange("p (s o) -> p s o", s=SLICES), in_=g_chunk, mul=-0.125)
-
         def find_top(ch):
             ch["top"] = next_round.tile([P, GROUPS], F32, name="top")
             nc.vector.tensor_reduce(out=ch["top"][:], in_=groups_of(ch["e"][:]), axis=AXIS.X, op=ALU.max)
@@ -116,7 +111,7 @@ def tile_pnn_v_kernel(tc, x, centers, probs, grad_out, out):
             nc.vector.tensor_tensor(out=ch["n2"][:], in0=ch["n4"][:, :, 0:2], in1=ch["n4"][:, :, 2:4], op=ALU.add)
 
         def count_2_to_1(ch):
-            ch["n"] = field("n")
+            ch["n"] = work.tile([P, GROUPS], BF16, name="n")
             nc.vector.tensor_tensor(
                 out=ch["n"][:].unsqueeze(2), in0=ch["n2"][:, :, 0:1], in1=ch["n2"][:, :, 1:2], op=ALU.add
             )
@@ -126,6 +121,14 @@ def tile_pnn_v_kernel(tc, x, centers, probs, grad_out, out):
             nc.scalar.activation(out=nn[:], in_=ch["n"][:], func=ACT.Square)
             ch["guess"] = field("guess")
             nc.scalar.activation(out=ch["guess"][:], in_=nn[:], func=ACT.Abs_reciprocal_sqrt)
+
+        def expand_n(ch):
+            ch["n_full"] = work.tile([P, GROUPS, ND], BF16, name="n_full")
+            nc.scalar.copy(out=ch["n_full"][:], in_=over_group(ch["n"][:]))
+
+        def nine_tops(ch):
+            ch["nine"] = work.tile([P, GROUPS, ND], BF16, name="nine")
+            nc.scalar.mul(out=ch["nine"][:], in_=ch["is_top"][:], mul=9.0)
 
         def newton_1(ch):
             ch["ng"] = field("ng")
@@ -137,25 +140,34 @@ def tile_pnn_v_kernel(tc, x, centers, probs, grad_out, out):
                 out=ch["neg_inv_n"][:], in0=ch["ng"][:], scalar=2.0, in1=ch["guess"][:], op0=ALU.subtract, op1=ALU.mult
             )
 
-        def share_top(ch):
-            ch["share"] = field("share")
+        def scale_g(ch):
+            g_chunk = g_raw[:].rearrange("p c t o -> p (c t) o")[:, :, ch["k"] * CHUNK_OUT : (ch["k"] + 1) * CHUNK_OUT]
+            ch["u"] = field("u")
             nc.vector.scalar_tensor_tensor(
-                out=ch["share"][:], in0=ch["neg_inv_n"][:], scalar=9.0, in1=ch["top"][:], op0=ALU.mult, op1=ALU.mult
+                out=ch["u"][:].rearrange("p (s o) -> p s o", s=SLICES),
+                in0=ch["neg_inv_n"][:].rearrange("p (s o) -> p s o", s=SLICES),
+                scalar=0.125,
+                in1=g_chunk,
+                op0=ALU.mult,
+                op1=ALU.mult,
             )
 
-        def place_share(ch):
-            ch["extra"] = work.tile([P, GROUPS, ND], F32, name="extra")
+        def weigh(ch):
+            ch["w"] = work.tile([P, GROUPS, ND], BF16, name="w")
             nc.vector.tensor_tensor(
-                out=ch["extra"][:], in0=ch["is_top"][:], in1=over_group(ch["share"][:]), op=ALU.mult
+                out=ch["w"][:].rearrange("p g d -> p (g d)"),
+                in0=ch["n_full"][:].rearrange("p g d -> p (g d)"),
+                in1=ch["nine"][:].rearrange("p g d -> p (g d)"),
+                op=ALU.subtract,
             )
-
-        def add_share(ch):
-            nc.vector.tensor_tensor(out=groups_of(ch["e"][:]), in0=groups_of(ch["e"][:]), in1=ch["extra"][:], op=ALU.add)
 
         def times_g(ch):
             nc.vector.tensor_tensor(
                 out=groups_of(ch["e"][:]), in0=groups_of(ch["e"][:]), in1=over_group(ch["u"][:]), op=ALU.mult
             )
+
+        def times_w(ch):
+            nc.vector.tensor_tensor(out=groups_of(ch["e"][:]), in0=groups_of(ch["e"][:]), in1=ch["w"][:], op=ALU.mult)
 
         def round_e(ch):
             ch["e_grouped"] = next_round.tile([P, PASSES, CHUNK, PACK], BF16, align_bytes=64, name="e_grouped")
@@ -200,6 +212,9 @@ def tile_pnn_v_kernel(tc, x, centers, probs, grad_out, out):
                             start=(s == 0),
                             stop=(s == SLICES - 1),
                         )
+            return r_sum
+
+        def negate(r_sum):
             neg_r = next_round.tile([P, HALVES * CHUNK_TILES], F32)
             nc.scalar.mul(out=neg_r[:], in_=r_sum[:, :, 0], mul=-1.0)
             return neg_r
@@ -244,15 +259,18 @@ def tile_pnn_v_kernel(tc, x, centers, probs, grad_out, out):
 
         last = []
         now = chunks_of(0)
-        both(scale_g, now)
         both(find_top, now)
         for rnd in range(ROUNDS + 1):
             after = chunks_of(rnd + 1) if rnd + 1 < ROUNDS else []
             both(mark_top, now)
+            both(nine_tops, now)
             both(count_8_to_4, now)
             both(count_4_to_2, now)
             both(count_2_to_1, now)
             both(guess_inverse, now)
+            both(expand_n, now)
+            if last:
+                neg_r = negate(r_sum)
             if rnd == 0:
                 x_grouped = regroup_x()
             if rnd == 1:
@@ -263,18 +281,17 @@ def tile_pnn_v_kernel(tc, x, centers, probs, grad_out, out):
             both(find_top, after)
             both(newton_1, now)
             both(newton_2, now)
-            both(share_top, now)
-            both(place_share, now)
+            both(scale_g, now)
+            both(weigh, now)
             if last:
                 finish(last[0], neg_r)
                 multiply(last[1])
-            both(add_share, now)
             both(times_g, now)
+            both(times_w, now)
             both(round_e, now)
             if last:
                 finish(last[1], neg_r)
             if now:
-                neg_r = sum_tokens(now)
-            both(scale_g, after)
+                r_sum = sum_tokens(now)
             last = now
             now = after

@@ -47,105 +47,123 @@ def groups_of(tile_ap):
     return tile_ap.rearrange("p c t (o d) -> p (c t o) d", d=ND)
 
 
+D_ON_GPSIMD = True
+
+
 def tile_pnn_v_kernel(tc, x, centers, probs, grad_out, out):
     nc = tc.nc
     centers_rows = centers.rearrange("o d i -> (o d) i")
     out_rows = out.rearrange("o d i -> (o d) i")
 
-    with tc.tile_pool(name="keep", bufs=1) as keep, tc.tile_pool(name="work", bufs=HALVES) as work, tc.tile_pool(
-        name="next_round", bufs=2 * HALVES
-    ) as next_round, tc.psum_pool(name="acc_pool", bufs=7) as acc_pool, tc.psum_pool(
+    with tc.tile_pool(name="keep", bufs=1) as keep, tc.tile_pool(name="two", bufs=HALVES) as two, tc.tile_pool(
+        name="four", bufs=2 * HALVES
+    ) as four, tc.psum_pool(name="acc_pool", bufs=7) as acc_pool, tc.psum_pool(
         name="sum_pool", bufs=1
     ) as sum_pool, tc.manual_schedule():
-        probs_sb = []
-        centers_sb = []
+        probs_sb = [keep.tile([P, PASSES, PACK, CHUNK], F32, name="probs%d" % k) for k in range(CHUNKS)]
+        centers_sb = [keep.tile([P, CHUNK_TILES, IN], BF16, name="centers%d" % k) for k in range(CHUNKS)]
         g_raw = keep.tile([P, PASSES, PACK, OUT], BF16)
         x_raw = keep.tile([P, PASSES, PACK, IN], BF16)
-        for k in range(CHUNKS):
+
+        def load_probs(k):
             cols = slice(k * CHUNK, (k + 1) * CHUNK)
-            pr = keep.tile([P, PASSES, PACK, CHUNK], F32, name="probs%d" % k)
             for c in range(PASSES):
                 tokens = slice(c * K_PASS, (c + 1) * K_PASS)
-                nc.sync.dma_start(out=pr[:, c], in_=probs[tokens, cols].rearrange("(p t) j -> p t j", t=PACK))
-            probs_sb.append(pr)
-            if k == HALVES - 1:
-                for c in range(PASSES):
-                    tokens = slice(c * K_PASS, (c + 1) * K_PASS)
-                    nc.sync.dma_start(out=g_raw[:, c], in_=grad_out[tokens, :].rearrange("(p t) o -> p t o", t=PACK))
-                for c in range(PASSES):
-                    tokens = slice(c * K_PASS, (c + 1) * K_PASS)
-                    nc.sync.dma_start(out=x_raw[:, c], in_=x[tokens, :].rearrange("(p t) i -> p t i", t=PACK))
-            cen = keep.tile([P, CHUNK_TILES, IN], BF16, name="centers%d" % k)
-            nc.sync.dma_start(out=cen[:], in_=centers_rows[cols, :].rearrange("(a p) i -> p a i", p=P))
-            centers_sb.append(cen)
+                nc.sync.dma_start(
+                    out=probs_sb[k][:, c], in_=probs[tokens, cols].rearrange("(p t) j -> p t j", t=PACK)
+                )
+
+        def load_centers(k):
+            cols = slice(k * CHUNK, (k + 1) * CHUNK)
+            nc.sync.dma_start(out=centers_sb[k][:], in_=centers_rows[cols, :].rearrange("(a p) i -> p a i", p=P))
+
+        def load_tokens(tile_sb, source):
+            for c in range(PASSES):
+                tokens = slice(c * K_PASS, (c + 1) * K_PASS)
+                nc.sync.dma_start(out=tile_sb[:, c], in_=source[tokens, :].rearrange("(p t) w -> p t w", t=PACK))
+
+        load_probs(0)
+        load_probs(1)
+        load_tokens(g_raw, grad_out)
+        load_probs(2)
+        load_probs(3)
+        load_tokens(x_raw, x)
+        for k in range(0, CHUNKS, HALVES):
+            load_centers(k)
+            load_centers(k + 1)
+            if k + 2 * HALVES < CHUNKS:
+                load_probs(k + 2 * HALVES)
+                load_probs(k + 2 * HALVES + 1)
 
         ones = keep.tile([P, ONES], F32)
         nc.vector.memset(ones[:], 1.0)
         x_codes = keep.tile([P, PASSES, IN], U32, align_bytes=64)
         x_scales = keep.tile([P, PASSES, IN], U8, align_bytes=64)
 
-        def field(name):
-            return work.tile([P, GROUPS], F32, name=name)
-
         def both(step, chunks):
             return [step(chunk) for chunk in chunks]
 
+        def flat(tile_ap):
+            return tile_ap.rearrange("p g d -> p (g d)")
+
+        def by_slice(field_ap):
+            return field_ap.rearrange("p (s o) -> p s o", s=SLICES)
+
         def find_top(ch):
-            ch["top"] = next_round.tile([P, GROUPS], F32, name="top")
+            ch["top"] = four.tile([P, GROUPS], F32, name="top")
             nc.vector.tensor_reduce(out=ch["top"][:], in_=groups_of(ch["e"][:]), axis=AXIS.X, op=ALU.max)
 
         def mark_top(ch):
-            ch["is_top"] = work.tile([P, GROUPS, ND], BF16, name="is_top")
+            ch["is_top"] = four.tile([P, GROUPS, ND], BF16, name="is_top")
             nc.vector.tensor_tensor(
                 out=ch["is_top"][:], in0=groups_of(ch["e"][:]), in1=over_group(ch["top"][:]), op=ALU.is_equal
             )
 
         def count_8_to_4(ch):
-            ch["n4"] = work.tile([P, GROUPS, 4], BF16, name="n4")
+            ch["n4"] = two.tile([P, GROUPS, 4], BF16, name="n4")
             nc.vector.tensor_tensor(
                 out=ch["n4"][:], in0=ch["is_top"][:, :, 0:4], in1=ch["is_top"][:, :, 4:8], op=ALU.add
             )
 
         def count_4_to_2(ch):
-            ch["n2"] = work.tile([P, GROUPS, 2], BF16, name="n2")
+            ch["n2"] = two.tile([P, GROUPS, 2], BF16, name="n2")
             nc.vector.tensor_tensor(out=ch["n2"][:], in0=ch["n4"][:, :, 0:2], in1=ch["n4"][:, :, 2:4], op=ALU.add)
 
         def count_2_to_1(ch):
-            ch["n"] = work.tile([P, GROUPS], BF16, name="n")
+            ch["n"] = four.tile([P, GROUPS], BF16, name="n")
             nc.vector.tensor_tensor(
                 out=ch["n"][:].unsqueeze(2), in0=ch["n2"][:, :, 0:1], in1=ch["n2"][:, :, 1:2], op=ALU.add
             )
 
+        def nine_tops(ch):
+            nc.scalar.mul(out=ch["is_top"][:], in_=ch["is_top"][:], mul=9.0)
+
         def guess_inverse(ch):
-            nn = field("nn")
+            nn = two.tile([P, GROUPS], F32, name="nn")
             nc.scalar.activation(out=nn[:], in_=ch["n"][:], func=ACT.Square)
-            ch["guess"] = field("guess")
+            ch["guess"] = four.tile([P, GROUPS], F32, name="guess")
             nc.scalar.activation(out=ch["guess"][:], in_=nn[:], func=ACT.Abs_reciprocal_sqrt)
 
         def expand_n(ch):
-            ch["n_full"] = work.tile([P, GROUPS, ND], BF16, name="n_full")
-            nc.scalar.copy(out=ch["n_full"][:], in_=over_group(ch["n"][:]))
-
-        def nine_tops(ch):
-            ch["nine"] = work.tile([P, GROUPS, ND], BF16, name="nine")
-            nc.scalar.mul(out=ch["nine"][:], in_=ch["is_top"][:], mul=9.0)
+            ch["w"] = four.tile([P, GROUPS, ND], BF16, name="w")
+            nc.scalar.copy(out=ch["w"][:], in_=over_group(ch["n"][:]))
 
         def newton_1(ch):
-            ch["ng"] = field("ng")
+            ch["ng"] = two.tile([P, GROUPS], F32, name="ng")
             nc.vector.tensor_tensor(out=ch["ng"][:], in0=ch["n"][:], in1=ch["guess"][:], op=ALU.mult)
 
         def newton_2(ch):
-            ch["neg_inv_n"] = field("neg_inv_n")
+            ch["neg_inv_n"] = two.tile([P, GROUPS], F32, name="neg_inv_n")
             nc.vector.scalar_tensor_tensor(
                 out=ch["neg_inv_n"][:], in0=ch["ng"][:], scalar=2.0, in1=ch["guess"][:], op0=ALU.subtract, op1=ALU.mult
             )
 
         def scale_g(ch):
             g_chunk = g_raw[:].rearrange("p c t o -> p (c t) o")[:, :, ch["k"] * CHUNK_OUT : (ch["k"] + 1) * CHUNK_OUT]
-            ch["u"] = field("u")
+            ch["u"] = two.tile([P, GROUPS], F32, name="u")
             nc.vector.scalar_tensor_tensor(
-                out=ch["u"][:].rearrange("p (s o) -> p s o", s=SLICES),
-                in0=ch["neg_inv_n"][:].rearrange("p (s o) -> p s o", s=SLICES),
+                out=by_slice(ch["u"][:]),
+                in0=by_slice(ch["neg_inv_n"][:]),
                 scalar=0.125,
                 in1=g_chunk,
                 op0=ALU.mult,
@@ -153,30 +171,27 @@ def tile_pnn_v_kernel(tc, x, centers, probs, grad_out, out):
             )
 
         def weigh(ch):
-            ch["w"] = work.tile([P, GROUPS, ND], BF16, name="w")
-            nc.vector.tensor_tensor(
-                out=ch["w"][:].rearrange("p g d -> p (g d)"),
-                in0=ch["n_full"][:].rearrange("p g d -> p (g d)"),
-                in1=ch["nine"][:].rearrange("p g d -> p (g d)"),
-                op=ALU.subtract,
-            )
+            nc.vector.tensor_tensor(out=flat(ch["w"][:]), in0=flat(ch["w"][:]), in1=flat(ch["is_top"][:]), op=ALU.subtract)
 
         def times_g(ch):
             nc.vector.tensor_tensor(
                 out=groups_of(ch["e"][:]), in0=groups_of(ch["e"][:]), in1=over_group(ch["u"][:]), op=ALU.mult
             )
 
-        def times_w(ch):
-            nc.vector.tensor_tensor(out=groups_of(ch["e"][:]), in0=groups_of(ch["e"][:]), in1=ch["w"][:], op=ALU.mult)
+        def times_w_on(engine):
+            def times_w(ch):
+                engine.tensor_tensor(out=groups_of(ch["e"][:]), in0=groups_of(ch["e"][:]), in1=ch["w"][:], op=ALU.mult)
+
+            return times_w
 
         def round_e(ch):
-            ch["e_grouped"] = next_round.tile([P, PASSES, CHUNK, PACK], BF16, align_bytes=64, name="e_grouped")
+            ch["e_grouped"] = two.tile([P, PASSES, CHUNK, PACK], BF16, align_bytes=64, name="e_grouped")
             for c in range(PASSES):
                 regroup(nc, ch["e_grouped"][:, c], ch["e"][:, c])
 
         def quantise_e(ch):
-            ch["codes"] = next_round.tile([P, PASSES, CHUNK], U32, align_bytes=64, name="e_codes")
-            ch["scales"] = next_round.tile([P, PASSES, CHUNK], U8, align_bytes=64, name="e_scales")
+            ch["codes"] = two.tile([P, PASSES, CHUNK], U32, align_bytes=64, name="e_codes")
+            ch["scales"] = two.tile([P, PASSES, CHUNK], U8, align_bytes=64, name="e_scales")
             nc.vector.quantize_mx(
                 out=ch["codes"][:].rearrange("p c j -> p (c j)").bitcast(E5M2_X4),
                 scales=ch["scales"][:].rearrange("p c j -> p (c j)"),
@@ -215,7 +230,7 @@ def tile_pnn_v_kernel(tc, x, centers, probs, grad_out, out):
             return r_sum
 
         def negate(r_sum):
-            neg_r = next_round.tile([P, HALVES * CHUNK_TILES], F32)
+            neg_r = two.tile([P, HALVES * CHUNK_TILES], F32)
             nc.scalar.mul(out=neg_r[:], in_=r_sum[:, :, 0], mul=-1.0)
             return neg_r
 
@@ -239,7 +254,7 @@ def tile_pnn_v_kernel(tc, x, centers, probs, grad_out, out):
                     ch["acc"].append((a, n_cols, acc))
 
         def finish(ch, neg_r):
-            results = [next_round.tile([P, IN], F32, name="result") for a in range(CHUNK_TILES)]
+            results = [four.tile([P, IN], F32, name="result") for a in range(CHUNK_TILES)]
             for a, n_cols, acc in ch["acc"]:
                 col = (ch["k"] % HALVES) * CHUNK_TILES + a
                 nc.vector.scalar_tensor_tensor(
@@ -254,44 +269,40 @@ def tile_pnn_v_kernel(tc, x, centers, probs, grad_out, out):
                 first = ch["k"] * CHUNK + a * M_TILE
                 nc.sync.dma_start(out=out_rows[first : first + M_TILE, :], in_=results[a][:])
 
-        def chunks_of(rnd):
-            return [{"k": rnd * HALVES + i, "e": probs_sb[rnd * HALVES + i]} for i in range(HALVES)]
+        rounds = [[{"k": rnd * HALVES + i, "e": probs_sb[rnd * HALVES + i]} for i in range(HALVES)] for rnd in range(ROUNDS)]
 
-        last = []
-        now = chunks_of(0)
-        both(find_top, now)
-        for rnd in range(ROUNDS + 1):
-            after = chunks_of(rnd + 1) if rnd + 1 < ROUNDS else []
-            both(mark_top, now)
-            both(nine_tops, now)
-            both(count_8_to_4, now)
-            both(count_4_to_2, now)
-            both(count_2_to_1, now)
-            both(guess_inverse, now)
-            both(expand_n, now)
-            if last:
-                neg_r = negate(r_sum)
-            if rnd == 0:
+        def chunks_of(rnd):
+            return rounds[rnd] if 0 <= rnd < ROUNDS else []
+
+        both(find_top, chunks_of(0))
+        r_sums = {}
+        for rnd in range(-1, ROUNDS + 1):
+            done, now, soon, later = chunks_of(rnd - 1), chunks_of(rnd), chunks_of(rnd + 1), chunks_of(rnd + 2)
+            both(mark_top, soon)
+            both(count_8_to_4, soon)
+            both(nine_tops, soon)
+            both(count_4_to_2, soon)
+            both(count_2_to_1, soon)
+            both(guess_inverse, soon)
+            both(expand_n, soon)
+            if rnd == -1:
                 x_grouped = regroup_x()
             if rnd == 1:
                 quantise_x(x_grouped)
-            both(quantise_e, last)
-            if last:
-                multiply(last[0])
-            both(find_top, after)
+            both(quantise_e, done)
+            both(multiply, done)
             both(newton_1, now)
             both(newton_2, now)
             both(scale_g, now)
             both(weigh, now)
-            if last:
-                finish(last[0], neg_r)
-                multiply(last[1])
             both(times_g, now)
-            both(times_w, now)
+            on_gpsimd = D_ON_GPSIMD and rnd < ROUNDS - 1
+            both(times_w_on(nc.gpsimd if on_gpsimd else nc.vector), now)
+            both(find_top, later)
+            if done:
+                neg_r = negate(r_sums[rnd - 1])
+            for ch in done:
+                finish(ch, neg_r)
             both(round_e, now)
-            if last:
-                finish(last[1], neg_r)
             if now:
-                r_sum = sum_tokens(now)
-            last = now
-            now = after
+                r_sums[rnd] = sum_tokens(now)

@@ -1,4 +1,5 @@
 import concourse.mybir as mybir
+from concourse.masks import make_identity
 
 F32 = mybir.dt.float32
 BF16 = mybir.dt.bfloat16
@@ -47,9 +48,6 @@ def groups_of(tile_ap):
     return tile_ap.rearrange("p c t (o d) -> p (c t o) d", d=ND)
 
 
-D_ON_GPSIMD = True
-
-
 def tile_pnn_v_kernel(tc, x, centers, probs, grad_out, out):
     nc = tc.nc
     centers_rows = centers.rearrange("o d i -> (o d) i")
@@ -57,7 +55,7 @@ def tile_pnn_v_kernel(tc, x, centers, probs, grad_out, out):
 
     with tc.tile_pool(name="keep", bufs=1) as keep, tc.tile_pool(name="two", bufs=HALVES) as two, tc.tile_pool(
         name="four", bufs=2 * HALVES
-    ) as four, tc.psum_pool(name="acc_pool", bufs=7) as acc_pool, tc.psum_pool(
+    ) as four, tc.psum_pool(name="acc_pool", bufs=5) as acc_pool, tc.psum_pool(
         name="sum_pool", bufs=1
     ) as sum_pool, tc.manual_schedule():
         probs_sb = [keep.tile([P, PASSES, PACK, CHUNK], F32, name="probs%d" % k) for k in range(CHUNKS)]
@@ -95,6 +93,8 @@ def tile_pnn_v_kernel(tc, x, centers, probs, grad_out, out):
                 load_probs(k + 2 * HALVES)
                 load_probs(k + 2 * HALVES + 1)
 
+        identity = keep.tile([P, P], F32)
+        make_identity(nc, identity[:])
         ones = keep.tile([P, ONES], F32)
         nc.vector.memset(ones[:], 1.0)
         x_codes = keep.tile([P, PASSES, IN], U32, align_bytes=64)
@@ -109,6 +109,12 @@ def tile_pnn_v_kernel(tc, x, centers, probs, grad_out, out):
         def by_slice(field_ap):
             return field_ap.rearrange("p (s o) -> p s o", s=SLICES)
 
+        def to_psum(chunks, key):
+            bank = sum_pool.tile([P, HALVES, GROUPS], F32, name=key + "_bank")
+            for i, ch in enumerate(chunks):
+                nc.tensor.matmul(out=bank[:, i, :], lhsT=identity[:], rhs=ch[key][:], start=True, stop=True)
+                ch[key + "_ps"] = bank[:, i, :]
+
         def find_top(ch):
             ch["top"] = four.tile([P, GROUPS], F32, name="top")
             nc.vector.tensor_reduce(out=ch["top"][:], in_=groups_of(ch["e"][:]), axis=AXIS.X, op=ALU.max)
@@ -116,7 +122,7 @@ def tile_pnn_v_kernel(tc, x, centers, probs, grad_out, out):
         def mark_top(ch):
             ch["is_top"] = four.tile([P, GROUPS, ND], BF16, name="is_top")
             nc.vector.tensor_tensor(
-                out=ch["is_top"][:], in0=groups_of(ch["e"][:]), in1=over_group(ch["top"][:]), op=ALU.is_equal
+                out=ch["is_top"][:], in0=groups_of(ch["e"][:]), in1=over_group(ch["top_ps"]), op=ALU.is_equal
             )
 
         def count_8_to_4(ch):
@@ -175,7 +181,7 @@ def tile_pnn_v_kernel(tc, x, centers, probs, grad_out, out):
 
         def times_g(ch):
             nc.vector.tensor_tensor(
-                out=groups_of(ch["e"][:]), in0=groups_of(ch["e"][:]), in1=over_group(ch["u"][:]), op=ALU.mult
+                out=groups_of(ch["e"][:]), in0=groups_of(ch["e"][:]), in1=over_group(ch["u_ps"]), op=ALU.mult
             )
 
         def times_w_on(engine):
@@ -274,7 +280,11 @@ def tile_pnn_v_kernel(tc, x, centers, probs, grad_out, out):
         def chunks_of(rnd):
             return rounds[rnd] if 0 <= rnd < ROUNDS else []
 
+        def on_gpsimd(rnd, i):
+            return rnd <= 1 or i == 0
+
         both(find_top, chunks_of(0))
+        to_psum(chunks_of(0), "top")
         r_sums = {}
         for rnd in range(-1, ROUNDS + 1):
             done, now, soon, later = chunks_of(rnd - 1), chunks_of(rnd), chunks_of(rnd + 1), chunks_of(rnd + 2)
@@ -287,22 +297,34 @@ def tile_pnn_v_kernel(tc, x, centers, probs, grad_out, out):
             both(expand_n, soon)
             if rnd == -1:
                 x_grouped = regroup_x()
-            if rnd == 1:
-                quantise_x(x_grouped)
-            both(quantise_e, done)
-            both(multiply, done)
             both(newton_1, now)
             both(newton_2, now)
             both(scale_g, now)
+            if now:
+                to_psum(now, "u")
+            if rnd == 1:
+                quantise_x(x_grouped)
+            for ch in done[:1]:
+                quantise_e(ch)
+                multiply(ch)
             both(weigh, now)
+            for ch in done[1:]:
+                quantise_e(ch)
+                multiply(ch)
             both(times_g, now)
-            on_gpsimd = D_ON_GPSIMD and rnd < ROUNDS - 1
-            both(times_w_on(nc.gpsimd if on_gpsimd else nc.vector), now)
+            for i, ch in enumerate(now):
+                if on_gpsimd(rnd, i):
+                    times_w_on(nc.gpsimd)(ch)
             both(find_top, later)
+            if later:
+                to_psum(later, "top")
             if done:
                 neg_r = negate(r_sums[rnd - 1])
             for ch in done:
                 finish(ch, neg_r)
+            for i, ch in enumerate(now):
+                if not on_gpsimd(rnd, i):
+                    times_w_on(nc.vector)(ch)
             both(round_e, now)
             if now:
                 r_sums[rnd] = sum_tokens(now)

@@ -53,9 +53,9 @@ def tile_pnn_v_kernel(tc, x, centers, probs, grad_out, out):
     centers_rows = centers.rearrange("o d i -> (o d) i")
     out_rows = out.rearrange("o d i -> (o d) i")
 
-    with tc.tile_pool(name="keep", bufs=1) as keep, tc.tile_pool(name="two", bufs=HALVES) as two, tc.tile_pool(
-        name="four", bufs=2 * HALVES
-    ) as four, tc.psum_pool(name="acc_pool", bufs=5) as acc_pool, tc.psum_pool(
+    with tc.tile_pool(name="keep", bufs=1) as keep, tc.tile_pool(name="two", bufs=2) as two, tc.tile_pool(
+        name="four", bufs=3
+    ) as four, tc.tile_pool(name="outs", bufs=4) as outs, tc.psum_pool(name="acc_pool", bufs=6) as acc_pool, tc.psum_pool(
         name="sum_pool", bufs=1
     ) as sum_pool, tc.manual_schedule():
         probs_sb = [keep.tile([P, PASSES, PACK, CHUNK], F32, name="probs%d" % k) for k in range(CHUNKS)]
@@ -75,23 +75,22 @@ def tile_pnn_v_kernel(tc, x, centers, probs, grad_out, out):
             cols = slice(k * CHUNK, (k + 1) * CHUNK)
             nc.sync.dma_start(out=centers_sb[k][:], in_=centers_rows[cols, :].rearrange("(a p) i -> p a i", p=P))
 
-        def load_tokens(tile_sb, source):
-            for c in range(PASSES):
-                tokens = slice(c * K_PASS, (c + 1) * K_PASS)
-                nc.sync.dma_start(out=tile_sb[:, c], in_=source[tokens, :].rearrange("(p t) w -> p t w", t=PACK))
+        def load_tokens(tile_sb, source, c):
+            tokens = slice(c * K_PASS, (c + 1) * K_PASS)
+            nc.sync.dma_start(out=tile_sb[:, c], in_=source[tokens, :].rearrange("(p t) w -> p t w", t=PACK))
 
         load_probs(0)
         load_probs(1)
-        load_tokens(g_raw, grad_out)
+        load_tokens(x_raw, x, 0)
         load_probs(2)
+        load_tokens(g_raw, grad_out, 0)
+        load_tokens(g_raw, grad_out, 1)
+        load_tokens(x_raw, x, 1)
         load_probs(3)
-        load_tokens(x_raw, x)
-        for k in range(0, CHUNKS, HALVES):
+        for k in range(CHUNKS):
+            if k + 4 < CHUNKS:
+                load_probs(k + 4)
             load_centers(k)
-            load_centers(k + 1)
-            if k + 2 * HALVES < CHUNKS:
-                load_probs(k + 2 * HALVES)
-                load_probs(k + 2 * HALVES + 1)
 
         identity = keep.tile([P, P], F32)
         make_identity(nc, identity[:])
@@ -109,11 +108,9 @@ def tile_pnn_v_kernel(tc, x, centers, probs, grad_out, out):
         def by_slice(field_ap):
             return field_ap.rearrange("p (s o) -> p s o", s=SLICES)
 
-        def to_psum(chunks, key):
-            bank = sum_pool.tile([P, HALVES, GROUPS], F32, name=key + "_bank")
-            for i, ch in enumerate(chunks):
-                nc.tensor.matmul(out=bank[:, i, :], lhsT=identity[:], rhs=ch[key][:], start=True, stop=True)
-                ch[key + "_ps"] = bank[:, i, :]
+        def top_to_psum(ch):
+            ch["top_ps"] = sum_pool.tile([P, GROUPS], F32, name="top_ps")
+            nc.tensor.matmul(out=ch["top_ps"][:], lhsT=identity[:], rhs=ch["top"][:], start=True, stop=True)
 
         def find_top(ch):
             ch["top"] = four.tile([P, GROUPS], F32, name="top")
@@ -122,7 +119,7 @@ def tile_pnn_v_kernel(tc, x, centers, probs, grad_out, out):
         def mark_top(ch):
             ch["is_top"] = four.tile([P, GROUPS, ND], BF16, name="is_top")
             nc.vector.tensor_tensor(
-                out=ch["is_top"][:], in0=groups_of(ch["e"][:]), in1=over_group(ch["top_ps"]), op=ALU.is_equal
+                out=ch["is_top"][:], in0=groups_of(ch["e"][:]), in1=over_group(ch["top_ps"][:]), op=ALU.is_equal
             )
 
         def count_8_to_4(ch):
@@ -181,7 +178,7 @@ def tile_pnn_v_kernel(tc, x, centers, probs, grad_out, out):
 
         def times_g(ch):
             nc.vector.tensor_tensor(
-                out=groups_of(ch["e"][:]), in0=groups_of(ch["e"][:]), in1=over_group(ch["u_ps"]), op=ALU.mult
+                out=groups_of(ch["e"][:]), in0=groups_of(ch["e"][:]), in1=over_group(ch["u"][:]), op=ALU.mult
             )
 
         def times_w_on(engine):
@@ -204,41 +201,48 @@ def tile_pnn_v_kernel(tc, x, centers, probs, grad_out, out):
                 in_=ch["e_grouped"][:].rearrange("p c j t -> p (c j t)"),
             )
 
-        def regroup_x():
-            grouped = []
-            for c in range(PASSES):
-                x_grouped = keep.tile([P, IN, PACK], BF16, align_bytes=64, name="x_grouped%d" % c)
-                regroup(nc, x_grouped[:], x_raw[:, c])
-                grouped.append(x_grouped)
-            return grouped
+        x_grouped = [keep.tile([P, IN, PACK], BF16, align_bytes=64, name="x_grouped%d" % c) for c in range(PASSES)]
 
-        def quantise_x(grouped):
+        def regroup_x(c):
+            for h in range(IN // N_TILE):
+                n_cols = slice(h * N_TILE, (h + 1) * N_TILE)
+                regroup(nc, x_grouped[c][:, n_cols, :], x_raw[:, c, :, n_cols])
+
+        def quantise_x():
             for c in range(PASSES):
                 nc.vector.quantize_mx(
                     out=x_codes[:, c].bitcast(E4M3_X4),
                     scales=x_scales[:, c],
-                    in_=grouped[c][:].rearrange("p i t -> p (i t)"),
+                    in_=x_grouped[c][:].rearrange("p i t -> p (i t)"),
                 )
 
-        def sum_tokens(chunks):
-            r_sum = sum_pool.tile([P, HALVES * CHUNK_TILES, ONES], F32)
-            for ch in chunks:
-                for a in range(CHUNK_TILES):
-                    col = (ch["k"] % HALVES) * CHUNK_TILES + a
-                    for s in range(SLICES):
-                        nc.tensor.matmul(
-                            out=r_sum[:, col, :],
-                            lhsT=ch["e"][:, s // PACK, s % PACK, a * M_TILE : (a + 1) * M_TILE],
-                            rhs=ones[:],
-                            start=(s == 0),
-                            stop=(s == SLICES - 1),
-                        )
-            return r_sum
+        def sum_tokens(ch, slices):
+            ch["r_sum"] = sum_pool.tile([P, CHUNK_TILES, ONES], F32, name="r_sum")
+            for a in range(CHUNK_TILES):
+                for s, part in enumerate(slices):
+                    nc.tensor.matmul(
+                        out=ch["r_sum"][:, a, :],
+                        lhsT=part[:, a * M_TILE : (a + 1) * M_TILE],
+                        rhs=ones[:],
+                        start=(s == 0),
+                        stop=(s == len(slices) - 1),
+                    )
 
-        def negate(r_sum):
-            neg_r = two.tile([P, HALVES * CHUNK_TILES], F32)
-            nc.scalar.mul(out=neg_r[:], in_=r_sum[:, :, 0], mul=-1.0)
-            return neg_r
+        def all_slices(ch):
+            return [ch["e"][:, s // PACK, s % PACK, :] for s in range(SLICES)]
+
+        def add_slices(ch):
+            half = keep.tile([P, PACK, CHUNK], F32, name="half")
+            nc.vector.tensor_tensor(out=half[:], in0=ch["e"][:, 0], in1=ch["e"][:, 1], op=ALU.add)
+            quarter = keep.tile([P, 2, CHUNK], F32, name="quarter")
+            nc.vector.tensor_tensor(out=quarter[:], in0=half[:, 0:2], in1=half[:, 2:4], op=ALU.add)
+            eighth = keep.tile([P, CHUNK], F32, name="eighth")
+            nc.vector.tensor_tensor(out=eighth[:], in0=quarter[:, 0], in1=quarter[:, 1], op=ALU.add)
+            return [eighth[:]]
+
+        def negate(ch):
+            ch["neg_r"] = two.tile([P, CHUNK_TILES], F32, name="neg_r")
+            nc.scalar.mul(out=ch["neg_r"][:], in_=ch["r_sum"][:, :, 0], mul=-1.0)
 
         def multiply(ch):
             ch["acc"] = []
@@ -259,14 +263,13 @@ def tile_pnn_v_kernel(tc, x, centers, probs, grad_out, out):
                         )
                     ch["acc"].append((a, n_cols, acc))
 
-        def finish(ch, neg_r):
-            results = [four.tile([P, IN], F32, name="result") for a in range(CHUNK_TILES)]
+        def finish(ch):
+            results = [outs.tile([P, IN], F32, name="result") for a in range(CHUNK_TILES)]
             for a, n_cols, acc in ch["acc"]:
-                col = (ch["k"] % HALVES) * CHUNK_TILES + a
                 nc.vector.scalar_tensor_tensor(
                     out=results[a][:, n_cols],
                     in0=centers_sb[ch["k"]][:, a, n_cols],
-                    scalar=neg_r[:, col : col + 1],
+                    scalar=ch["neg_r"][:, a : a + 1],
                     in1=acc[:],
                     op0=ALU.mult,
                     op1=ALU.add,
@@ -275,56 +278,42 @@ def tile_pnn_v_kernel(tc, x, centers, probs, grad_out, out):
                 first = ch["k"] * CHUNK + a * M_TILE
                 nc.sync.dma_start(out=out_rows[first : first + M_TILE, :], in_=results[a][:])
 
-        rounds = [[{"k": rnd * HALVES + i, "e": probs_sb[rnd * HALVES + i]} for i in range(HALVES)] for rnd in range(ROUNDS)]
+        chunks = [{"k": k, "e": probs_sb[k]} for k in range(CHUNKS)]
+        LAST = CHUNKS - 1
 
-        def chunks_of(rnd):
-            return rounds[rnd] if 0 <= rnd < ROUNDS else []
+        def at(k):
+            return chunks[k : k + 1] if k >= 0 else []
 
-        def on_gpsimd(rnd, i):
-            return rnd <= 1 or i == 0
-
-        both(find_top, chunks_of(0))
-        to_psum(chunks_of(0), "top")
-        r_sums = {}
-        for rnd in range(-1, ROUNDS + 1):
-            done, now, soon, later = chunks_of(rnd - 1), chunks_of(rnd), chunks_of(rnd + 1), chunks_of(rnd + 2)
-            both(mark_top, soon)
+        for k in range(-3, CHUNKS + 1):
+            done, now, soon = at(k - 1), at(k), at(k + 1)
             both(count_8_to_4, soon)
             both(nine_tops, soon)
+            both(newton_1, now)
             both(count_4_to_2, soon)
+            both(newton_2, now)
             both(count_2_to_1, soon)
             both(guess_inverse, soon)
             both(expand_n, soon)
-            if rnd == -1:
-                x_grouped = regroup_x()
-            both(newton_1, now)
-            both(newton_2, now)
             both(scale_g, now)
-            if now:
-                to_psum(now, "u")
-            if rnd == 1:
-                quantise_x(x_grouped)
-            for ch in done[:1]:
-                quantise_e(ch)
-                multiply(ch)
+            if k == -2:
+                regroup_x(0)
+            if k == 0:
+                regroup_x(1)
+            if k == 1:
+                quantise_x()
             both(weigh, now)
-            for ch in done[1:]:
-                quantise_e(ch)
-                multiply(ch)
+            both(quantise_e, done)
+            both(multiply, done)
             both(times_g, now)
-            for i, ch in enumerate(now):
-                if on_gpsimd(rnd, i):
-                    times_w_on(nc.gpsimd)(ch)
-            both(find_top, later)
-            if later:
-                to_psum(later, "top")
-            if done:
-                neg_r = negate(r_sums[rnd - 1])
-            for ch in done:
-                finish(ch, neg_r)
-            for i, ch in enumerate(now):
-                if not on_gpsimd(rnd, i):
-                    times_w_on(nc.vector)(ch)
+            if k < LAST:
+                both(times_w_on(nc.gpsimd), now)
+            both(find_top, at(k + 3))
+            both(mark_top, at(k + 2))
+            both(top_to_psum, at(k + 3))
+            both(negate, done)
+            both(finish, done)
+            if k == LAST:
+                both(times_w_on(nc.vector), now)
             both(round_e, now)
-            if now:
-                r_sums[rnd] = sum_tokens(now)
+            for ch in now:
+                sum_tokens(ch, add_slices(ch) if k == LAST else all_slices(ch))

@@ -30,6 +30,8 @@ CHUNK_TILES = CHUNK // M_TILE
 ONES = 64
 RUN = 4
 
+HEAD_PIECES = 2
+
 FLOPS = 2 * TOKENS * ROWS * IN
 
 
@@ -63,13 +65,14 @@ def tile_pnn_v_kernel(tc, x, centers, probs, grad_out, out):
         g_raw = keep.tile([P, PASSES, PACK, OUT], BF16)
         x_raw = keep.tile([P, PASSES, PACK, IN], BF16)
 
-        def load_probs(k):
+        def load_probs(k, pieces=1):
             cols = slice(k * CHUNK, (k + 1) * CHUNK)
+            width = PACK // pieces
             for c in range(PASSES):
                 tokens = slice(c * K_PASS, (c + 1) * K_PASS)
-                nc.sync.dma_start(
-                    out=probs_sb[k][:, c], in_=probs[tokens, cols].rearrange("(p t) j -> p t j", t=PACK)
-                )
+                rows = probs[tokens, cols].rearrange("(p t) j -> p t j", t=PACK)
+                for t0 in range(0, PACK, width):
+                    nc.sync.dma_start(out=probs_sb[k][:, c, t0 : t0 + width], in_=rows[:, t0 : t0 + width, :])
 
         def load_centers(k):
             cols = slice(k * CHUNK, (k + 1) * CHUNK)
@@ -79,14 +82,14 @@ def tile_pnn_v_kernel(tc, x, centers, probs, grad_out, out):
             tokens = slice(c * K_PASS, (c + 1) * K_PASS)
             nc.sync.dma_start(out=tile_sb[:, c], in_=source[tokens, :].rearrange("(p t) w -> p t w", t=PACK))
 
-        load_probs(0)
-        load_probs(1)
-        load_tokens(x_raw, x, 0)
+        load_probs(0, HEAD_PIECES)
+        load_probs(1, HEAD_PIECES)
         load_probs(2)
         load_tokens(g_raw, grad_out, 0)
         load_tokens(g_raw, grad_out, 1)
-        load_tokens(x_raw, x, 1)
         load_probs(3)
+        load_tokens(x_raw, x, 0)
+        load_tokens(x_raw, x, 1)
         for k in range(CHUNKS):
             if k + 4 < CHUNKS:
                 load_probs(k + 4)
@@ -114,7 +117,12 @@ def tile_pnn_v_kernel(tc, x, centers, probs, grad_out, out):
 
         def find_top(ch):
             ch["top"] = four.tile([P, GROUPS], F32, name="top")
-            nc.vector.tensor_reduce(out=ch["top"][:], in_=groups_of(ch["e"][:]), axis=AXIS.X, op=ALU.max)
+            pieces = PASSES * HEAD_PIECES if ch["k"] < 2 else 1
+            step = GROUPS // pieces
+            for g0 in range(0, GROUPS, step):
+                nc.vector.tensor_reduce(
+                    out=ch["top"][:, g0 : g0 + step], in_=groups_of(ch["e"][:])[:, g0 : g0 + step, :], axis=AXIS.X, op=ALU.max
+                )
 
         def mark_top(ch):
             ch["is_top"] = four.tile([P, GROUPS, ND], BF16, name="is_top")
@@ -285,7 +293,8 @@ def tile_pnn_v_kernel(tc, x, centers, probs, grad_out, out):
             return chunks[k : k + 1] if k >= 0 else []
 
         for k in range(-3, CHUNKS + 1):
-            done, now, soon = at(k - 1), at(k), at(k + 1)
+            ended, now, soon = at(k - 1), at(k), at(k + 1)
+            done = [] if k == 1 else (at(0) + at(1) if k == 2 else ended)
             both(count_8_to_4, soon)
             both(nine_tops, soon)
             both(newton_1, now)
@@ -295,11 +304,11 @@ def tile_pnn_v_kernel(tc, x, centers, probs, grad_out, out):
             both(guess_inverse, soon)
             both(expand_n, soon)
             both(scale_g, now)
-            if k == -2:
-                regroup_x(0)
             if k == 0:
-                regroup_x(1)
+                regroup_x(0)
             if k == 1:
+                regroup_x(1)
+            if k == 2:
                 quantise_x()
             both(weigh, now)
             both(quantise_e, done)
@@ -310,7 +319,7 @@ def tile_pnn_v_kernel(tc, x, centers, probs, grad_out, out):
             both(find_top, at(k + 3))
             both(mark_top, at(k + 2))
             both(top_to_psum, at(k + 3))
-            both(negate, done)
+            both(negate, ended)
             both(finish, done)
             if k == LAST:
                 both(times_w_on(nc.vector), now)

@@ -294,7 +294,9 @@ def tile_pnn_v_kernel(tc, x, centers, probs, grad_out, out):
 
         for k in range(-3, CHUNKS + 1):
             ended, now, soon = at(k - 1), at(k), at(k + 1)
-            done = [] if k == 1 else (at(0) + at(1) if k == 2 else ended)
+            done = at(k - 2) if k <= LAST - 1 else []
+            if k >= LAST - 1:
+                done = done + ended
             both(count_8_to_4, soon)
             both(nine_tops, soon)
             both(newton_1, now)

@@ -57,7 +57,7 @@ def tile_pnn_v_kernel(tc, x, centers, probs, grad_out, out):
 
     with tc.tile_pool(name="keep", bufs=1) as keep, tc.tile_pool(name="two", bufs=2) as two, tc.tile_pool(
         name="four", bufs=3
-    ) as four, tc.tile_pool(name="outs", bufs=4) as outs, tc.psum_pool(name="acc_pool", bufs=6) as acc_pool, tc.psum_pool(
+    ) as four, tc.tile_pool(name="outs", bufs=4) as outs, tc.psum_pool(name="acc_pool", bufs=5) as acc_pool, tc.psum_pool(
         name="sum_pool", bufs=1
     ) as sum_pool, tc.manual_schedule():
         probs_sb = [keep.tile([P, PASSES, PACK, CHUNK], F32, name="probs%d" % k) for k in range(CHUNKS)]
@@ -114,6 +114,10 @@ def tile_pnn_v_kernel(tc, x, centers, probs, grad_out, out):
         def top_to_psum(ch):
             ch["top_ps"] = sum_pool.tile([P, GROUPS], F32, name="top_ps")
             nc.tensor.matmul(out=ch["top_ps"][:], lhsT=identity[:], rhs=ch["top"][:], start=True, stop=True)
+
+        def u_to_psum(ch):
+            ch["u_ps"] = sum_pool.tile([P, GROUPS], F32, name="u_ps")
+            nc.tensor.matmul(out=ch["u_ps"][:], lhsT=identity[:], rhs=ch["u"][:], start=True, stop=True)
 
         def find_top(ch):
             ch["top"] = four.tile([P, GROUPS], F32, name="top")
@@ -184,9 +188,22 @@ def tile_pnn_v_kernel(tc, x, centers, probs, grad_out, out):
         def weigh(ch):
             nc.vector.tensor_tensor(out=flat(ch["w"][:]), in0=flat(ch["w"][:]), in1=flat(ch["is_top"][:]), op=ALU.subtract)
 
-        def times_g(ch):
+        def times_g(ch, share):
+            cut = GROUPS - share
             nc.vector.tensor_tensor(
-                out=groups_of(ch["e"][:]), in0=groups_of(ch["e"][:]), in1=over_group(ch["u"][:]), op=ALU.mult
+                out=groups_of(ch["e"][:])[:, :cut, :],
+                in0=groups_of(ch["e"][:])[:, :cut, :],
+                in1=ch["u_ps"][:, :cut].unsqueeze(2).to_broadcast([P, cut, ND]),
+                op=ALU.mult,
+            )
+
+        def times_g_rest(ch, share):
+            cut = GROUPS - share
+            nc.gpsimd.tensor_tensor(
+                out=groups_of(ch["e"][:])[:, cut:, :],
+                in0=groups_of(ch["e"][:])[:, cut:, :],
+                in1=ch["u"][:, cut:].unsqueeze(2).to_broadcast([P, share, ND]),
+                op=ALU.mult,
             )
 
         def times_w_on(engine):
@@ -292,11 +309,11 @@ def tile_pnn_v_kernel(tc, x, centers, probs, grad_out, out):
         def at(k):
             return chunks[k : k + 1] if k >= 0 else []
 
-        for k in range(-3, CHUNKS + 1):
-            ended, now, soon = at(k - 1), at(k), at(k + 1)
-            done = at(k - 2) if k <= LAST - 1 else []
-            if k >= LAST - 1:
-                done = done + ended
+        def gpsimd_share(k):
+            return GROUPS // 2 if 2 <= k <= 4 else 0
+
+        for k in range(-3, CHUNKS + 2):
+            done, ended, now, soon = at(k - 2), at(k - 1), at(k), at(k + 1)
             both(count_8_to_4, soon)
             both(nine_tops, soon)
             both(newton_1, now)
@@ -306,25 +323,35 @@ def tile_pnn_v_kernel(tc, x, centers, probs, grad_out, out):
             both(guess_inverse, soon)
             both(expand_n, soon)
             both(scale_g, now)
+            both(u_to_psum, now)
             if k == 0:
                 regroup_x(0)
             if k == 1:
                 regroup_x(1)
             if k == 2:
                 quantise_x()
-            both(weigh, now)
+            both(weigh, ended)
+            if k - 1 == LAST:
+                both(times_w_on(nc.vector), ended)
             both(quantise_e, done)
             both(multiply, done)
-            both(times_g, now)
-            if k < LAST:
-                both(times_w_on(nc.gpsimd), now)
+            if k - 1 < LAST:
+                both(times_w_on(nc.gpsimd), ended)
+            for ch in now:
+                if gpsimd_share(k):
+                    times_g_rest(ch, gpsimd_share(k))
+            if k - 1 == LAST:
+                both(round_e, ended)
+                for ch in ended:
+                    sum_tokens(ch, add_slices(ch))
             both(find_top, at(k + 3))
             both(mark_top, at(k + 2))
             both(top_to_psum, at(k + 3))
-            both(negate, ended)
+            both(negate, done)
             both(finish, done)
-            if k == LAST:
-                both(times_w_on(nc.vector), now)
-            both(round_e, now)
             for ch in now:
-                sum_tokens(ch, add_slices(ch) if k == LAST else all_slices(ch))
+                times_g(ch, gpsimd_share(k))
+            if k - 1 < LAST:
+                both(round_e, ended)
+                for ch in ended:
+                    sum_tokens(ch, all_slices(ch))

@@ -333,8 +333,9 @@ def tile_pnn_v_kernel(tc, x, centers, probs, grad_out, out):
             both(weigh, ended)
             if k - 1 == LAST:
                 both(times_w_on(nc.vector), ended)
-            both(quantise_e, done)
-            both(multiply, done)
+            if k - 2 < LAST:
+                both(quantise_e, done)
+                both(multiply, done)
             if k - 1 < LAST:
                 both(times_w_on(nc.gpsimd), ended)
             for ch in now:
@@ -344,6 +345,8 @@ def tile_pnn_v_kernel(tc, x, centers, probs, grad_out, out):
                 both(round_e, ended)
                 for ch in ended:
                     sum_tokens(ch, add_slices(ch))
+                both(quantise_e, ended)
+                both(multiply, ended)
             both(find_top, at(k + 3))
             both(mark_top, at(k + 2))
             both(top_to_psum, at(k + 3))

@@ -151,7 +151,7 @@ def tile_pnn_v_kernel(tc, x, centers, probs, grad_out, out):
             )
 
         def nine_tops(ch):
-            nc.scalar.mul(out=ch["is_top"][:], in_=ch["is_top"][:], mul=9.0)
+            nc.scalar.mul(out=ch["is_top"][:], in_=ch["is_top"][:], mul=1.125)
 
         def guess_inverse(ch):
             nn = two.tile([P, GROUPS], F32, name="nn")
@@ -161,28 +161,21 @@ def tile_pnn_v_kernel(tc, x, centers, probs, grad_out, out):
 
         def expand_n(ch):
             ch["w"] = four.tile([P, GROUPS, ND], BF16, name="w")
-            nc.scalar.copy(out=ch["w"][:], in_=over_group(ch["n"][:]))
+            nc.scalar.mul(out=ch["w"][:], in_=over_group(ch["n"][:]), mul=0.125)
 
         def newton_1(ch):
             ch["ng"] = two.tile([P, GROUPS], F32, name="ng")
             nc.vector.tensor_tensor(out=ch["ng"][:], in0=ch["n"][:], in1=ch["guess"][:], op=ALU.mult)
 
-        def newton_2(ch):
-            ch["neg_inv_n"] = two.tile([P, GROUPS], F32, name="neg_inv_n")
-            nc.vector.scalar_tensor_tensor(
-                out=ch["neg_inv_n"][:], in0=ch["ng"][:], scalar=2.0, in1=ch["guess"][:], op0=ALU.subtract, op1=ALU.mult
-            )
+        def guess_times_g(ch):
+            g_chunk = g_raw[:].rearrange("p c t o -> p (c t) o")[:, :, ch["k"] * CHUNK_OUT : (ch["k"] + 1) * CHUNK_OUT]
+            ch["gg"] = four.tile([P, GROUPS], F32, name="gg")
+            nc.gpsimd.tensor_tensor(out=by_slice(ch["gg"][:]), in0=by_slice(ch["guess"][:]), in1=g_chunk, op=ALU.mult)
 
         def scale_g(ch):
-            g_chunk = g_raw[:].rearrange("p c t o -> p (c t) o")[:, :, ch["k"] * CHUNK_OUT : (ch["k"] + 1) * CHUNK_OUT]
             ch["u"] = two.tile([P, GROUPS], F32, name="u")
             nc.vector.scalar_tensor_tensor(
-                out=by_slice(ch["u"][:]),
-                in0=by_slice(ch["neg_inv_n"][:]),
-                scalar=0.125,
-                in1=g_chunk,
-                op0=ALU.mult,
-                op1=ALU.mult,
+                out=ch["u"][:], in0=ch["ng"][:], scalar=2.0, in1=ch["gg"][:], op0=ALU.subtract, op1=ALU.mult
             )
 
         def weigh(ch):
@@ -299,9 +292,8 @@ def tile_pnn_v_kernel(tc, x, centers, probs, grad_out, out):
                     op0=ALU.mult,
                     op1=ALU.add,
                 )
-            for a in range(CHUNK_TILES):
                 first = ch["k"] * CHUNK + a * M_TILE
-                nc.sync.dma_start(out=out_rows[first : first + M_TILE, :], in_=results[a][:])
+                nc.sync.dma_start(out=out_rows[first : first + M_TILE, n_cols], in_=results[a][:, n_cols])
 
         chunks = [{"k": k, "e": probs_sb[k]} for k in range(CHUNKS)]
         LAST = CHUNKS - 1
@@ -310,7 +302,11 @@ def tile_pnn_v_kernel(tc, x, centers, probs, grad_out, out):
             return chunks[k : k + 1] if k >= 0 else []
 
         def gpsimd_share(k):
-            return GROUPS // 2 if 2 <= k <= 4 else 0
+            if k == 0:
+                return 3 * GROUPS // 4
+            if 2 <= k <= 4:
+                return GROUPS // 2
+            return GROUPS // 4 if k in (1, 5) else 0
 
         for k in range(-3, CHUNKS + 2):
             done, ended, now, soon = at(k - 2), at(k - 1), at(k), at(k + 1)
@@ -318,12 +314,11 @@ def tile_pnn_v_kernel(tc, x, centers, probs, grad_out, out):
             both(nine_tops, soon)
             both(newton_1, now)
             both(count_4_to_2, soon)
-            both(newton_2, now)
+            both(scale_g, now)
+            both(u_to_psum, now)
             both(count_2_to_1, soon)
             both(guess_inverse, soon)
             both(expand_n, soon)
-            both(scale_g, now)
-            both(u_to_psum, now)
             if k == 0:
                 regroup_x(0)
             if k == 1:
@@ -341,6 +336,7 @@ def tile_pnn_v_kernel(tc, x, centers, probs, grad_out, out):
             for ch in now:
                 if gpsimd_share(k):
                     times_g_rest(ch, gpsimd_share(k))
+            both(guess_times_g, soon)
             if k - 1 == LAST:
                 both(round_e, ended)
                 for ch in ended:

@@ -97,8 +97,8 @@ def tile_pnn_v_kernel(tc, x, centers, probs, grad_out, out):
 
         identity = keep.tile([P, P], F32)
         make_identity(nc, identity[:])
-        ones = keep.tile([P, ONES], F32)
-        nc.vector.memset(ones[:], 1.0)
+        identity_16 = keep.tile([P, P], BF16)
+        nc.scalar.copy(out=identity_16[:], in_=identity[:])
         x_codes = keep.tile([P, PASSES, IN], U32, align_bytes=64)
         x_scales = keep.tile([P, PASSES, IN], U8, align_bytes=64)
 
@@ -140,15 +140,12 @@ def tile_pnn_v_kernel(tc, x, centers, probs, grad_out, out):
                 out=ch["n4"][:], in0=ch["is_top"][:, :, 0:4], in1=ch["is_top"][:, :, 4:8], op=ALU.add
             )
 
-        def count_4_to_2(ch):
-            ch["n2"] = two.tile([P, GROUPS, 2], BF16, name="n2")
-            nc.vector.tensor_tensor(out=ch["n2"][:], in0=ch["n4"][:, :, 0:2], in1=ch["n4"][:, :, 2:4], op=ALU.add)
-
-        def count_2_to_1(ch):
-            ch["n"] = four.tile([P, GROUPS], BF16, name="n")
-            nc.vector.tensor_tensor(
-                out=ch["n"][:].unsqueeze(2), in0=ch["n2"][:, :, 0:1], in1=ch["n2"][:, :, 1:2], op=ALU.add
-            )
+        def count_4_to_1(ch):
+            ch["n"] = sum_pool.tile([P, GROUPS], F32, name="n_ps")
+            for i in range(4):
+                nc.tensor.matmul(
+                    out=ch["n"][:], lhsT=identity_16[:], rhs=ch["n4"][:, :, i], start=(i == 0), stop=(i == 3)
+                )
 
         def nine_tops(ch):
             nc.scalar.mul(out=ch["is_top"][:], in_=ch["is_top"][:], mul=1.125)
@@ -178,8 +175,10 @@ def tile_pnn_v_kernel(tc, x, centers, probs, grad_out, out):
                 out=ch["u"][:], in0=ch["ng"][:], scalar=2.0, in1=ch["gg"][:], op0=ALU.subtract, op1=ALU.mult
             )
 
-        def weigh(ch):
-            nc.vector.tensor_tensor(out=flat(ch["w"][:]), in0=flat(ch["w"][:]), in1=flat(ch["is_top"][:]), op=ALU.subtract)
+        def weigh(ch, passes=range(PASSES)):
+            groups = slice(passes.start * GROUPS // PASSES, passes.stop * GROUPS // PASSES)
+            w = flat(ch["w"][:, groups, :])
+            nc.vector.tensor_tensor(out=w, in0=w, in1=flat(ch["is_top"][:, groups, :]), op=ALU.subtract)
 
         def times_g(ch, share):
             cut = GROUPS - share
@@ -199,16 +198,21 @@ def tile_pnn_v_kernel(tc, x, centers, probs, grad_out, out):
                 op=ALU.mult,
             )
 
-        def times_w_on(engine):
-            def times_w(ch):
-                engine.tensor_tensor(out=groups_of(ch["e"][:]), in0=groups_of(ch["e"][:]), in1=ch["w"][:], op=ALU.mult)
-
-            return times_w
+        def times_w(ch, engine, passes):
+            groups = slice(passes.start * GROUPS // PASSES, passes.stop * GROUPS // PASSES)
+            e = groups_of(ch["e"][:])[:, groups, :]
+            engine.tensor_tensor(out=e, in0=e, in1=ch["w"][:, groups, :], op=ALU.mult)
 
         def round_e(ch):
-            ch["e_grouped"] = two.tile([P, PASSES, CHUNK, PACK], BF16, align_bytes=64, name="e_grouped")
+            start_round(ch)
             for c in range(PASSES):
-                regroup(nc, ch["e_grouped"][:, c], ch["e"][:, c])
+                round_pass(ch, c)
+
+        def start_round(ch):
+            ch["e_grouped"] = two.tile([P, PASSES, CHUNK, PACK], BF16, align_bytes=64, name="e_grouped")
+
+        def round_pass(ch, c):
+            regroup(nc, ch["e_grouped"][:, c], ch["e"][:, c])
 
         def quantise_e(ch):
             ch["codes"] = two.tile([P, PASSES, CHUNK], U32, align_bytes=64, name="e_codes")
@@ -226,41 +230,30 @@ def tile_pnn_v_kernel(tc, x, centers, probs, grad_out, out):
                 n_cols = slice(h * N_TILE, (h + 1) * N_TILE)
                 regroup(nc, x_grouped[c][:, n_cols, :], x_raw[:, c, :, n_cols])
 
-        def quantise_x():
-            for c in range(PASSES):
-                nc.vector.quantize_mx(
-                    out=x_codes[:, c].bitcast(E4M3_X4),
-                    scales=x_scales[:, c],
-                    in_=x_grouped[c][:].rearrange("p i t -> p (i t)"),
-                )
+        def quantise_x(c):
+            nc.vector.quantize_mx(
+                out=x_codes[:, c].bitcast(E4M3_X4),
+                scales=x_scales[:, c],
+                in_=x_grouped[c][:].rearrange("p i t -> p (i t)"),
+            )
 
-        def sum_tokens(ch, slices):
-            ch["r_sum"] = sum_pool.tile([P, CHUNK_TILES, ONES], F32, name="r_sum")
+        def turn(out, block, start, stop):
+            nc.tensor.matmul(out=out, lhsT=block, rhs=identity[:], is_transpose=True, start=start, stop=stop)
+
+        def sum_tokens(ch):
+            ch["sums"] = acc_pool.tile([P, CHUNK_TILES, P], F32, name="acc")
             for a in range(CHUNK_TILES):
-                for s, part in enumerate(slices):
-                    nc.tensor.matmul(
-                        out=ch["r_sum"][:, a, :],
-                        lhsT=part[:, a * M_TILE : (a + 1) * M_TILE],
-                        rhs=ones[:],
-                        start=(s == 0),
-                        stop=(s == len(slices) - 1),
-                    )
-
-        def all_slices(ch):
-            return [ch["e"][:, s // PACK, s % PACK, :] for s in range(SLICES)]
-
-        def add_slices(ch):
-            half = keep.tile([P, PACK, CHUNK], F32, name="half")
-            nc.vector.tensor_tensor(out=half[:], in0=ch["e"][:, 0], in1=ch["e"][:, 1], op=ALU.add)
-            quarter = keep.tile([P, 2, CHUNK], F32, name="quarter")
-            nc.vector.tensor_tensor(out=quarter[:], in0=half[:, 0:2], in1=half[:, 2:4], op=ALU.add)
-            eighth = keep.tile([P, CHUNK], F32, name="eighth")
-            nc.vector.tensor_tensor(out=eighth[:], in0=quarter[:, 0], in1=quarter[:, 1], op=ALU.add)
-            return [eighth[:]]
+                for s in range(SLICES):
+                    block = ch["e"][:, s // PACK, s % PACK, a * M_TILE : (a + 1) * M_TILE]
+                    turn(ch["sums"][:, a, :], block, s == 0, s == SLICES - 1)
 
         def negate(ch):
             ch["neg_r"] = two.tile([P, CHUNK_TILES], F32, name="neg_r")
-            nc.scalar.mul(out=ch["neg_r"][:], in_=ch["r_sum"][:, :, 0], mul=-1.0)
+            for a in range(CHUNK_TILES):
+                scrap = two.tile([P, P], F32, name="scrap")
+                nc.scalar.activation(
+                    out=scrap[:], in_=ch["sums"][:, a, :], func=ACT.Copy, scale=-1.0, accum_out=ch["neg_r"][:, a : a + 1]
+                )
 
         def multiply(ch):
             ch["acc"] = []
@@ -268,7 +261,7 @@ def tile_pnn_v_kernel(tc, x, centers, probs, grad_out, out):
                 rows = slice(a * M_TILE, (a + 1) * M_TILE)
                 for h in range(IN // N_TILE):
                     n_cols = slice(h * N_TILE, (h + 1) * N_TILE)
-                    acc = acc_pool.tile([P, N_TILE], F32)
+                    acc = acc_pool.tile([P, N_TILE], F32, name="acc")
                     for c in range(PASSES):
                         nc.tensor.matmul_mx(
                             out=acc[:],
@@ -310,47 +303,73 @@ def tile_pnn_v_kernel(tc, x, centers, probs, grad_out, out):
 
         for k in range(-3, CHUNKS + 2):
             done, ended, now, soon = at(k - 2), at(k - 1), at(k), at(k + 1)
+            drain = k >= LAST - 1
             both(count_8_to_4, soon)
             both(nine_tops, soon)
             both(newton_1, now)
-            both(count_4_to_2, soon)
+            both(count_4_to_1, soon)
             both(scale_g, now)
             both(u_to_psum, now)
-            both(count_2_to_1, soon)
             both(guess_inverse, soon)
+            if k - 1 != LAST:
+                both(negate, done)
             both(expand_n, soon)
-            if k == 0:
-                regroup_x(0)
-            if k == 1:
-                regroup_x(1)
+            if k in (0, 1):
+                regroup_x(k)
             if k == 2:
-                quantise_x()
-            both(weigh, ended)
+                quantise_x(0)
             if k - 1 == LAST:
-                both(times_w_on(nc.vector), ended)
-            if k - 2 < LAST:
-                both(quantise_e, done)
-                both(multiply, done)
-            if k - 1 < LAST:
-                both(times_w_on(nc.gpsimd), ended)
+                for ch in ended:
+                    weigh(ch, range(0, 1))
+                    times_w(ch, nc.vector, range(0, 1))
+                    both(quantise_e, done)
+                    both(multiply, done)
+                    weigh(ch, range(1, PASSES))
+                    times_w(ch, nc.gpsimd, range(1, PASSES))
+                    start_round(ch)
+                    round_pass(ch, 0)
+                    both(negate, done)
+                    round_pass(ch, 1)
+                    sum_tokens(ch)
+            elif k - 2 < LAST:
+                if k == LAST - 1:
+                    both(quantise_e, done)
+                    both(multiply, done)
+                    both(weigh, ended)
+                elif k == LAST:
+                    for ch in ended:
+                        weigh(ch, range(0, 1))
+                        both(quantise_e, done)
+                        both(multiply, done)
+                        weigh(ch, range(1, PASSES))
+                else:
+                    both(weigh, ended)
+                    if k != 2:
+                        both(quantise_e, done)
+                        both(multiply, done)
+                for ch in ended:
+                    times_w(ch, nc.gpsimd, range(0, PASSES))
             for ch in now:
                 if gpsimd_share(k):
                     times_g_rest(ch, gpsimd_share(k))
             both(guess_times_g, soon)
-            if k - 1 == LAST:
-                both(round_e, ended)
-                for ch in ended:
-                    sum_tokens(ch, add_slices(ch))
-                both(quantise_e, ended)
-                both(multiply, ended)
             both(find_top, at(k + 3))
             both(mark_top, at(k + 2))
             both(top_to_psum, at(k + 3))
-            both(negate, done)
+            if k == 2:
+                quantise_x(1)
+                both(quantise_e, done)
+                both(multiply, done)
+            if drain or k == 2:
+                for ch in now:
+                    times_g(ch, gpsimd_share(k))
             both(finish, done)
-            for ch in now:
-                times_g(ch, gpsimd_share(k))
+            if k - 1 == LAST:
+                both(quantise_e, ended)
+                both(multiply, ended)
+            if not (drain or k == 2):
+                for ch in now:
+                    times_g(ch, gpsimd_share(k))
             if k - 1 < LAST:
                 both(round_e, ended)
-                for ch in ended:
-                    sum_tokens(ch, all_slices(ch))
+                both(sum_tokens, ended)

@@ -304,12 +304,13 @@ def tile_pnn_v_kernel(tc, x, centers, probs, grad_out, out):
         for k in range(-3, CHUNKS + 2):
             done, ended, now, soon = at(k - 2), at(k - 1), at(k), at(k + 1)
             drain = k >= LAST - 1
+            both(newton_1, now)
             both(count_8_to_4, soon)
             both(nine_tops, soon)
-            both(newton_1, now)
             both(count_4_to_1, soon)
-            both(scale_g, now)
-            both(u_to_psum, now)
+            if k != LAST:
+                both(scale_g, now)
+                both(u_to_psum, now)
             both(guess_inverse, soon)
             if k - 1 != LAST:
                 both(negate, done)
@@ -338,17 +339,23 @@ def tile_pnn_v_kernel(tc, x, centers, probs, grad_out, out):
                     both(weigh, ended)
                 elif k == LAST:
                     for ch in ended:
-                        weigh(ch, range(0, 1))
-                        both(quantise_e, done)
-                        both(multiply, done)
                         weigh(ch, range(1, PASSES))
+                        both(quantise_e, done)
+                        both(scale_g, now)
+                        both(u_to_psum, now)
+                        both(multiply, done)
+                        weigh(ch, range(0, 1))
                 else:
                     both(weigh, ended)
                     if k != 2:
                         both(quantise_e, done)
                         both(multiply, done)
                 for ch in ended:
-                    times_w(ch, nc.gpsimd, range(0, PASSES))
+                    if drain:
+                        times_w(ch, nc.gpsimd, range(0, 1))
+                        times_w(ch, nc.gpsimd, range(1, PASSES))
+                    else:
+                        times_w(ch, nc.gpsimd, range(0, PASSES))
             for ch in now:
                 if gpsimd_share(k):
                     times_g_rest(ch, gpsimd_share(k))

@@ -28,6 +28,7 @@ HALVES = 2
 ROUNDS = CHUNKS // HALVES
 CHUNK_TILES = CHUNK // M_TILE
 ONES = 64
+TURNED = range(2, 6)
 RUN = 4
 
 HEAD_PIECES = 2
@@ -82,14 +83,22 @@ def tile_pnn_v_kernel(tc, x, centers, probs, grad_out, out):
             tokens = slice(c * K_PASS, (c + 1) * K_PASS)
             nc.sync.dma_start(out=tile_sb[:, c], in_=source[tokens, :].rearrange("(p t) w -> p t w", t=PACK))
 
+        def load_x(c, h):
+            rows = x[c * K_PASS : (c + 1) * K_PASS, h * N_TILE : (h + 1) * N_TILE]
+            nc.sync.dma_start(
+                out=x_raw[:, c, :, h * N_TILE : (h + 1) * N_TILE], in_=rows.rearrange("(p t) w -> p t w", t=PACK)
+            )
+
         load_probs(0, HEAD_PIECES)
         load_probs(1, HEAD_PIECES)
+        load_x(0, 0)
         load_probs(2)
         load_tokens(g_raw, grad_out, 0)
         load_tokens(g_raw, grad_out, 1)
         load_probs(3)
-        load_tokens(x_raw, x, 0)
-        load_tokens(x_raw, x, 1)
+        load_x(0, 1)
+        load_x(1, 0)
+        load_x(1, 1)
         for k in range(CHUNKS):
             if k + 4 < CHUNKS:
                 load_probs(k + 4)
@@ -129,26 +138,36 @@ def tile_pnn_v_kernel(tc, x, centers, probs, grad_out, out):
                 )
 
         def mark_top(ch):
-            ch["is_top"] = four.tile([P, GROUPS, ND], BF16, name="is_top")
+            turned = ch["k"] in TURNED
+            ch["is_top"] = two.tile([P, GROUPS, ND], F32 if turned else BF16, name="is_top")
             nc.vector.tensor_tensor(
                 out=ch["is_top"][:], in0=groups_of(ch["e"][:]), in1=over_group(ch["top_ps"][:]), op=ALU.is_equal
             )
 
-        def count_8_to_4(ch):
-            ch["n4"] = two.tile([P, GROUPS, 4], BF16, name="n4")
-            nc.vector.tensor_tensor(
-                out=ch["n4"][:], in0=ch["is_top"][:, :, 0:4], in1=ch["is_top"][:, :, 4:8], op=ALU.add
-            )
-
-        def count_4_to_1(ch):
+        def count_by_products(ch):
             ch["n"] = sum_pool.tile([P, GROUPS], F32, name="n_ps")
-            for i in range(4):
+            for d in range(ND):
                 nc.tensor.matmul(
-                    out=ch["n"][:], lhsT=identity_16[:], rhs=ch["n4"][:, :, i], start=(i == 0), stop=(i == 3)
+                    out=ch["n"][:], lhsT=identity_16[:], rhs=ch["is_top"][:, :, d], start=(d == 0), stop=(d == ND - 1)
                 )
 
+        def count_turned(ch):
+            ch["n_turned"] = acc_pool.tile([P, GROUPS // P, P], F32, name="acc")
+            for h in range(GROUPS // P):
+                for d in range(ND):
+                    turn(ch["n_turned"][:, h, :], ch["is_top"][:, h * P : (h + 1) * P, d], d == 0, d == ND - 1)
+
+            ch["n_sb"] = two.tile([P, GROUPS // P, P], F32, name="n_sb")
+            nc.scalar.copy(out=ch["n_sb"][:], in_=ch["n_turned"][:])
+
+        def count_back(ch):
+            ch["n"] = sum_pool.tile([P, GROUPS], F32, name="n_ps")
+            for h in range(GROUPS // P):
+                turn(ch["n"][:, h * P : (h + 1) * P], ch["n_sb"][:, h, :], True, True)
+
         def nine_tops(ch):
-            nc.scalar.mul(out=ch["is_top"][:], in_=ch["is_top"][:], mul=1.125)
+            ch["nine"] = four.tile([P, GROUPS, ND], BF16, name="nine")
+            nc.scalar.mul(out=ch["nine"][:], in_=ch["is_top"][:], mul=1.125)
 
         def guess_inverse(ch):
             nn = two.tile([P, GROUPS], F32, name="nn")
@@ -178,7 +197,7 @@ def tile_pnn_v_kernel(tc, x, centers, probs, grad_out, out):
         def weigh(ch, passes=range(PASSES)):
             groups = slice(passes.start * GROUPS // PASSES, passes.stop * GROUPS // PASSES)
             w = flat(ch["w"][:, groups, :])
-            nc.vector.tensor_tensor(out=w, in0=w, in1=flat(ch["is_top"][:, groups, :]), op=ALU.subtract)
+            nc.vector.tensor_tensor(out=w, in0=w, in1=flat(ch["nine"][:, groups, :]), op=ALU.subtract)
 
         def times_g(ch, share):
             cut = GROUPS - share
@@ -225,10 +244,9 @@ def tile_pnn_v_kernel(tc, x, centers, probs, grad_out, out):
 
         x_grouped = [keep.tile([P, IN, PACK], BF16, align_bytes=64, name="x_grouped%d" % c) for c in range(PASSES)]
 
-        def regroup_x(c):
-            for h in range(IN // N_TILE):
-                n_cols = slice(h * N_TILE, (h + 1) * N_TILE)
-                regroup(nc, x_grouped[c][:, n_cols, :], x_raw[:, c, :, n_cols])
+        def regroup_x(c, h):
+            n_cols = slice(h * N_TILE, (h + 1) * N_TILE)
+            regroup(nc, x_grouped[c][:, n_cols, :], x_raw[:, c, :, n_cols])
 
         def quantise_x(c):
             nc.vector.quantize_mx(
@@ -274,9 +292,9 @@ def tile_pnn_v_kernel(tc, x, centers, probs, grad_out, out):
                         )
                     ch["acc"].append((a, n_cols, acc))
 
-        def finish(ch):
-            results = [outs.tile([P, IN], F32, name="result") for a in range(CHUNK_TILES)]
-            for a, n_cols, acc in ch["acc"]:
+        def finish(ch, tiles=range(CHUNK_TILES)):
+            results = {a: outs.tile([P, IN], F32, name="result") for a in tiles}
+            for a, n_cols, acc in [block for block in ch["acc"] if block[0] in tiles]:
                 nc.vector.scalar_tensor_tensor(
                     out=results[a][:, n_cols],
                     in0=centers_sb[ch["k"]][:, a, n_cols],
@@ -304,10 +322,13 @@ def tile_pnn_v_kernel(tc, x, centers, probs, grad_out, out):
         for k in range(-3, CHUNKS + 2):
             done, ended, now, soon = at(k - 2), at(k - 1), at(k), at(k + 1)
             drain = k >= LAST - 1
-            both(newton_1, now)
-            both(count_8_to_4, soon)
+            if k + 1 in TURNED:
+                both(count_turned, soon)
+            else:
+                both(count_by_products, soon)
+            if k + 1 in TURNED:
+                both(count_back, soon)
             both(nine_tops, soon)
-            both(count_4_to_1, soon)
             if k != LAST:
                 both(scale_g, now)
                 both(u_to_psum, now)
@@ -315,8 +336,13 @@ def tile_pnn_v_kernel(tc, x, centers, probs, grad_out, out):
             if k - 1 != LAST:
                 both(negate, done)
             both(expand_n, soon)
-            if k in (0, 1):
-                regroup_x(k)
+            if k == -2:
+                regroup_x(0, 0)
+            if k == 0:
+                regroup_x(0, 1)
+            if k == 1:
+                regroup_x(1, 0)
+                regroup_x(1, 1)
             if k == 2:
                 quantise_x(0)
             if k - 1 == LAST:
@@ -326,14 +352,14 @@ def tile_pnn_v_kernel(tc, x, centers, probs, grad_out, out):
                     both(quantise_e, done)
                     both(multiply, done)
                     weigh(ch, range(1, PASSES))
-                    times_w(ch, nc.gpsimd, range(1, PASSES))
+                    times_w(ch, nc.vector, range(1, PASSES))
                     start_round(ch)
                     round_pass(ch, 0)
                     both(negate, done)
                     round_pass(ch, 1)
                     sum_tokens(ch)
             elif k - 2 < LAST:
-                if k == LAST - 1:
+                if k != 2 and k != LAST:
                     both(quantise_e, done)
                     both(multiply, done)
                     both(weigh, ended)
@@ -347,9 +373,6 @@ def tile_pnn_v_kernel(tc, x, centers, probs, grad_out, out):
                         weigh(ch, range(0, 1))
                 else:
                     both(weigh, ended)
-                    if k != 2:
-                        both(quantise_e, done)
-                        both(multiply, done)
                 for ch in ended:
                     if drain:
                         times_w(ch, nc.gpsimd, range(0, 1))
@@ -370,10 +393,16 @@ def tile_pnn_v_kernel(tc, x, centers, probs, grad_out, out):
             if drain or k == 2:
                 for ch in now:
                     times_g(ch, gpsimd_share(k))
-            both(finish, done)
             if k - 1 == LAST:
+                for ch in done:
+                    finish(ch, range(0, 1))
                 both(quantise_e, ended)
+                for ch in done:
+                    finish(ch, range(1, CHUNK_TILES))
                 both(multiply, ended)
+            else:
+                both(finish, done)
+            both(newton_1, soon)
             if not (drain or k == 2):
                 for ch in now:
                     times_g(ch, gpsimd_share(k))

@@ -28,7 +28,6 @@ HALVES = 2
 ROUNDS = CHUNKS // HALVES
 CHUNK_TILES = CHUNK // M_TILE
 ONES = 64
-TURNED = range(2, 6)
 RUN = 4
 
 HEAD_PIECES = 2
@@ -64,7 +63,11 @@ def tile_pnn_v_kernel(tc, x, centers, probs, grad_out, out):
         probs_sb = [keep.tile([P, PASSES, PACK, CHUNK], F32, name="probs%d" % k) for k in range(CHUNKS)]
         centers_sb = [keep.tile([P, CHUNK_TILES, IN], BF16, name="centers%d" % k) for k in range(CHUNKS)]
         g_raw = keep.tile([P, PASSES, PACK, OUT], BF16)
-        x_raw = keep.tile([P, PASSES, PACK, IN], BF16)
+        x_raw = {
+            (c, h): keep.tile([P, PACK, N_TILE], BF16, name="x_raw%d%d" % (c, h))
+            for c in range(PASSES)
+            for h in range(IN // N_TILE)
+        }
 
         def load_probs(k, pieces=1):
             cols = slice(k * CHUNK, (k + 1) * CHUNK)
@@ -85,9 +88,7 @@ def tile_pnn_v_kernel(tc, x, centers, probs, grad_out, out):
 
         def load_x(c, h):
             rows = x[c * K_PASS : (c + 1) * K_PASS, h * N_TILE : (h + 1) * N_TILE]
-            nc.sync.dma_start(
-                out=x_raw[:, c, :, h * N_TILE : (h + 1) * N_TILE], in_=rows.rearrange("(p t) w -> p t w", t=PACK)
-            )
+            nc.sync.dma_start(out=x_raw[c, h][:], in_=rows.rearrange("(p t) w -> p t w", t=PACK))
 
         load_probs(0, HEAD_PIECES)
         load_probs(1, HEAD_PIECES)
@@ -138,36 +139,26 @@ def tile_pnn_v_kernel(tc, x, centers, probs, grad_out, out):
                 )
 
         def mark_top(ch):
-            turned = ch["k"] in TURNED
-            ch["is_top"] = two.tile([P, GROUPS, ND], F32 if turned else BF16, name="is_top")
+            ch["is_top"] = four.tile([P, GROUPS, ND], BF16, name="is_top")
             nc.vector.tensor_tensor(
                 out=ch["is_top"][:], in0=groups_of(ch["e"][:]), in1=over_group(ch["top_ps"][:]), op=ALU.is_equal
             )
 
-        def count_by_products(ch):
+        def count_8_to_4(ch):
+            ch["n4"] = two.tile([P, GROUPS, 4], BF16, name="n4")
+            nc.vector.tensor_tensor(
+                out=ch["n4"][:], in0=ch["is_top"][:, :, 0:4], in1=ch["is_top"][:, :, 4:8], op=ALU.add
+            )
+
+        def count_4_to_1(ch):
             ch["n"] = sum_pool.tile([P, GROUPS], F32, name="n_ps")
-            for d in range(ND):
+            for i in range(4):
                 nc.tensor.matmul(
-                    out=ch["n"][:], lhsT=identity_16[:], rhs=ch["is_top"][:, :, d], start=(d == 0), stop=(d == ND - 1)
+                    out=ch["n"][:], lhsT=identity_16[:], rhs=ch["n4"][:, :, i], start=(i == 0), stop=(i == 3)
                 )
 
-        def count_turned(ch):
-            ch["n_turned"] = acc_pool.tile([P, GROUPS // P, P], F32, name="acc")
-            for h in range(GROUPS // P):
-                for d in range(ND):
-                    turn(ch["n_turned"][:, h, :], ch["is_top"][:, h * P : (h + 1) * P, d], d == 0, d == ND - 1)
-
-            ch["n_sb"] = two.tile([P, GROUPS // P, P], F32, name="n_sb")
-            nc.scalar.copy(out=ch["n_sb"][:], in_=ch["n_turned"][:])
-
-        def count_back(ch):
-            ch["n"] = sum_pool.tile([P, GROUPS], F32, name="n_ps")
-            for h in range(GROUPS // P):
-                turn(ch["n"][:, h * P : (h + 1) * P], ch["n_sb"][:, h, :], True, True)
-
         def nine_tops(ch):
-            ch["nine"] = four.tile([P, GROUPS, ND], BF16, name="nine")
-            nc.scalar.mul(out=ch["nine"][:], in_=ch["is_top"][:], mul=1.125)
+            nc.scalar.mul(out=ch["is_top"][:], in_=ch["is_top"][:], mul=1.125)
 
         def guess_inverse(ch):
             nn = two.tile([P, GROUPS], F32, name="nn")
@@ -197,7 +188,7 @@ def tile_pnn_v_kernel(tc, x, centers, probs, grad_out, out):
         def weigh(ch, passes=range(PASSES)):
             groups = slice(passes.start * GROUPS // PASSES, passes.stop * GROUPS // PASSES)
             w = flat(ch["w"][:, groups, :])
-            nc.vector.tensor_tensor(out=w, in0=w, in1=flat(ch["nine"][:, groups, :]), op=ALU.subtract)
+            nc.vector.tensor_tensor(out=w, in0=w, in1=flat(ch["is_top"][:, groups, :]), op=ALU.subtract)
 
         def times_g(ch, share):
             cut = GROUPS - share
@@ -246,7 +237,7 @@ def tile_pnn_v_kernel(tc, x, centers, probs, grad_out, out):
 
         def regroup_x(c, h):
             n_cols = slice(h * N_TILE, (h + 1) * N_TILE)
-            regroup(nc, x_grouped[c][:, n_cols, :], x_raw[:, c, :, n_cols])
+            regroup(nc, x_grouped[c][:, n_cols, :], x_raw[c, h][:])
 
         def quantise_x(c):
             nc.vector.quantize_mx(
@@ -322,13 +313,9 @@ def tile_pnn_v_kernel(tc, x, centers, probs, grad_out, out):
         for k in range(-3, CHUNKS + 2):
             done, ended, now, soon = at(k - 2), at(k - 1), at(k), at(k + 1)
             drain = k >= LAST - 1
-            if k + 1 in TURNED:
-                both(count_turned, soon)
-            else:
-                both(count_by_products, soon)
-            if k + 1 in TURNED:
-                both(count_back, soon)
+            both(count_8_to_4, soon)
             both(nine_tops, soon)
+            both(count_4_to_1, soon)
             if k != LAST:
                 both(scale_g, now)
                 both(u_to_psum, now)

@@ -131,7 +131,7 @@ def tile_pnn_v_kernel(tc, x, centers, probs, grad_out, out):
 
         def find_top(ch):
             ch["top"] = four.tile([P, GROUPS], F32, name="top")
-            pieces = PASSES * HEAD_PIECES if ch["k"] < 2 else 1
+            pieces = PASSES * HEAD_PIECES if ch["k"] == 0 else 1
             step = GROUPS // pieces
             for g0 in range(0, GROUPS, step):
                 nc.vector.tensor_reduce(
@@ -141,7 +141,7 @@ def tile_pnn_v_kernel(tc, x, centers, probs, grad_out, out):
         def mark_top(ch):
             ch["is_top"] = four.tile([P, GROUPS, ND], BF16, name="is_top")
             nc.vector.tensor_tensor(
-                out=ch["is_top"][:], in0=groups_of(ch["e"][:]), in1=over_group(ch["top_ps"][:]), op=ALU.is_equal
+                out=ch["is_top"][:], in0=groups_of(ch["e"][:]), in1=over_group(ch["top_ps" if ch["k"] else "top"][:]), op=ALU.is_equal
             )
 
         def count_8_to_4(ch):
@@ -286,16 +286,20 @@ def tile_pnn_v_kernel(tc, x, centers, probs, grad_out, out):
         def finish(ch, tiles=range(CHUNK_TILES)):
             results = {a: outs.tile([P, IN], F32, name="result") for a in tiles}
             for a, n_cols, acc in [block for block in ch["acc"] if block[0] in tiles]:
-                nc.vector.scalar_tensor_tensor(
-                    out=results[a][:, n_cols],
-                    in0=centers_sb[ch["k"]][:, a, n_cols],
-                    scalar=ch["neg_r"][:, a : a + 1],
-                    in1=acc[:],
-                    op0=ALU.mult,
-                    op1=ALU.add,
-                )
                 first = ch["k"] * CHUNK + a * M_TILE
-                nc.sync.dma_start(out=out_rows[first : first + M_TILE, n_cols], in_=results[a][:, n_cols])
+                parts = 2 if first + M_TILE == ROWS and n_cols.stop == IN else 1
+                width = N_TILE // parts
+                for n0 in range(0, N_TILE, width):
+                    cols = slice(n_cols.start + n0, n_cols.start + n0 + width)
+                    nc.vector.scalar_tensor_tensor(
+                        out=results[a][:, cols],
+                        in0=centers_sb[ch["k"]][:, a, cols],
+                        scalar=ch["neg_r"][:, a : a + 1],
+                        in1=acc[:, n0 : n0 + width],
+                        op0=ALU.mult,
+                        op1=ALU.add,
+                    )
+                    nc.sync.dma_start(out=out_rows[first : first + M_TILE, cols], in_=results[a][:, cols])
 
         chunks = [{"k": k, "e": probs_sb[k]} for k in range(CHUNKS)]
         LAST = CHUNKS - 1
@@ -370,9 +374,14 @@ def tile_pnn_v_kernel(tc, x, centers, probs, grad_out, out):
                 if gpsimd_share(k):
                     times_g_rest(ch, gpsimd_share(k))
             both(guess_times_g, soon)
-            both(find_top, at(k + 3))
-            both(mark_top, at(k + 2))
-            both(top_to_psum, at(k + 3))
+            if k == -2:
+                both(mark_top, at(0))
+                both(find_top, at(1))
+            else:
+                both(find_top, at(k + 3))
+                both(mark_top, at(k + 2))
+            if k > -3:
+                both(top_to_psum, at(k + 3))
             if k == 2:
                 quantise_x(1)
                 both(quantise_e, done)

import concourse.mybir as mybir
from concourse.masks import make_identity

F32 = mybir.dt.float32
BF16 = mybir.dt.bfloat16
U32 = mybir.dt.uint32
U8 = mybir.dt.uint8
E4M3_X4 = mybir.dt.float8_e4m3fn_x4
E5M2_X4 = mybir.dt.float8_e5m2_x4
ALU = mybir.AluOpType
ACT = mybir.ActivationFunctionType
AXIS = mybir.AxisListType

TOKENS, IN, OUT, ND = 1024, 1024, 256, 8
ROWS = OUT * ND
P = 128
PACK = 4
K_PASS = P * PACK
PASSES = TOKENS // K_PASS
SLICES = PASSES * PACK
M_TILE = 128
N_TILE = 512
CHUNK = 256
CHUNKS = ROWS // CHUNK
CHUNK_OUT = CHUNK // ND
GROUPS = SLICES * CHUNK_OUT
HALVES = 2
ROUNDS = CHUNKS // HALVES
CHUNK_TILES = CHUNK // M_TILE
ONES = 64
RUN = 4

HEAD_PIECES = 2

FLOPS = 2 * TOKENS * ROWS * IN


def regroup(nc, grouped, rows):
    nc.scalar.copy(
        out=grouped.rearrange("p (a i) t -> p a t i", i=RUN),
        in_=rows.rearrange("p t (a i) -> p a t i", i=RUN),
    )


def over_group(field):
    return field.unsqueeze(2).to_broadcast([P, GROUPS, ND])


def groups_of(tile_ap):
    return tile_ap.rearrange("p c t (o d) -> p (c t o) d", d=ND)


def tile_pnn_v_kernel(tc, x, centers, probs, grad_out, out):
    nc = tc.nc
    centers_rows = centers.rearrange("o d i -> (o d) i")
    out_rows = out.rearrange("o d i -> (o d) i")

    with tc.tile_pool(name="keep", bufs=1) as keep, tc.tile_pool(name="two", bufs=2) as two, tc.tile_pool(
        name="four", bufs=3
    ) as four, tc.tile_pool(name="outs", bufs=4) as outs, tc.psum_pool(name="acc_pool", bufs=5) as acc_pool, tc.psum_pool(
        name="sum_pool", bufs=1
    ) as sum_pool, tc.manual_schedule():
        probs_sb = [keep.tile([P, PASSES, PACK, CHUNK], F32, name="probs%d" % k) for k in range(CHUNKS)]
        centers_sb = [keep.tile([P, CHUNK_TILES, IN], BF16, name="centers%d" % k) for k in range(CHUNKS)]
        g_raw = keep.tile([P, PASSES, PACK, OUT], BF16)
        x_raw = {
            (c, h): keep.tile([P, PACK, N_TILE], BF16, name="x_raw%d%d" % (c, h))
            for c in range(PASSES)
            for h in range(IN // N_TILE)
        }

        def load_probs(k, pieces=1):
            cols = slice(k * CHUNK, (k + 1) * CHUNK)
            width = PACK // pieces
            for c in range(PASSES):
                tokens = slice(c * K_PASS, (c + 1) * K_PASS)
                rows = probs[tokens, cols].rearrange("(p t) j -> p t j", t=PACK)
                for t0 in range(0, PACK, width):
                    nc.sync.dma_start(out=probs_sb[k][:, c, t0 : t0 + width], in_=rows[:, t0 : t0 + width, :])

        def load_centers(k):
            cols = slice(k * CHUNK, (k + 1) * CHUNK)
            nc.sync.dma_start(out=centers_sb[k][:], in_=centers_rows[cols, :].rearrange("(a p) i -> p a i", p=P))

        def load_tokens(tile_sb, source, c):
            tokens = slice(c * K_PASS, (c + 1) * K_PASS)
            nc.sync.dma_start(out=tile_sb[:, c], in_=source[tokens, :].rearrange("(p t) w -> p t w", t=PACK))

        def load_x(c, h):
            rows = x[c * K_PASS : (c + 1) * K_PASS, h * N_TILE : (h + 1) * N_TILE]
            nc.sync.dma_start(out=x_raw[c, h][:], in_=rows.rearrange("(p t) w -> p t w", t=PACK))

        load_probs(0, HEAD_PIECES)
        load_probs(1, HEAD_PIECES)
        load_x(0, 0)
        load_probs(2)
        load_tokens(g_raw, grad_out, 0)
        load_tokens(g_raw, grad_out, 1)
        load_probs(3)
        load_x(0, 1)
        load_x(1, 0)
        load_x(1, 1)
        for k in range(CHUNKS):
            if k + 4 < CHUNKS:
                load_probs(k + 4)
            load_centers(k)

        identity = keep.tile([P, P], F32)
        make_identity(nc, identity[:])
        identity_16 = keep.tile([P, P], BF16)
        nc.scalar.copy(out=identity_16[:], in_=identity[:])
        x_codes = keep.tile([P, PASSES, IN], U32, align_bytes=64)
        x_scales = keep.tile([P, PASSES, IN], U8, align_bytes=64)

        def both(step, chunks):
            return [step(chunk) for chunk in chunks]

        def flat(tile_ap):
            return tile_ap.rearrange("p g d -> p (g d)")

        def by_slice(field_ap):
            return field_ap.rearrange("p (s o) -> p s o", s=SLICES)

        def top_to_psum(ch):
            ch["top_ps"] = sum_pool.tile([P, GROUPS], F32, name="top_ps")
            nc.tensor.matmul(out=ch["top_ps"][:], lhsT=identity[:], rhs=ch["top"][:], start=True, stop=True)

        def u_to_psum(ch):
            ch["u_ps"] = sum_pool.tile([P, GROUPS], F32, name="u_ps")
            nc.tensor.matmul(out=ch["u_ps"][:], lhsT=identity[:], rhs=ch["u"][:], start=True, stop=True)

        def find_top(ch):
            ch["top"] = four.tile([P, GROUPS], F32, name="top")
            pieces = PASSES * HEAD_PIECES if ch["k"] == 0 else 1
            step = GROUPS // pieces
            for g0 in range(0, GROUPS, step):
                nc.vector.tensor_reduce(
                    out=ch["top"][:, g0 : g0 + step], in_=groups_of(ch["e"][:])[:, g0 : g0 + step, :], axis=AXIS.X, op=ALU.max
                )

        def mark_top(ch):
            ch["is_top"] = four.tile([P, GROUPS, ND], BF16, name="is_top")
            nc.vector.tensor_tensor(
                out=ch["is_top"][:], in0=groups_of(ch["e"][:]), in1=over_group(ch["top_ps" if ch["k"] else "top"][:]), op=ALU.is_equal
            )

        def count_8_to_4(ch):
            ch["n4"] = two.tile([P, GROUPS, 4], BF16, name="n4")
            nc.vector.tensor_tensor(
                out=ch["n4"][:], in0=ch["is_top"][:, :, 0:4], in1=ch["is_top"][:, :, 4:8], op=ALU.add
            )

        def count_4_to_1(ch):
            ch["n"] = sum_pool.tile([P, GROUPS], F32, name="n_ps")
            for i in range(4):
                nc.tensor.matmul(
                    out=ch["n"][:], lhsT=identity_16[:], rhs=ch["n4"][:, :, i], start=(i == 0), stop=(i == 3)
                )

        def nine_tops(ch):
            nc.scalar.mul(out=ch["is_top"][:], in_=ch["is_top"][:], mul=1.125)

        def guess_inverse(ch):
            nn = two.tile([P, GROUPS], F32, name="nn")
            nc.scalar.activation(out=nn[:], in_=ch["n"][:], func=ACT.Square)
            ch["guess"] = four.tile([P, GROUPS], F32, name="guess")
            nc.scalar.activation(out=ch["guess"][:], in_=nn[:], func=ACT.Abs_reciprocal_sqrt)

        def expand_n(ch):
            ch["w"] = four.tile([P, GROUPS, ND], BF16, name="w")
            nc.scalar.mul(out=ch["w"][:], in_=over_group(ch["n"][:]), mul=0.125)

        def newton_1(ch):
            ch["ng"] = two.tile([P, GROUPS], F32, name="ng")
            nc.vector.tensor_tensor(out=ch["ng"][:], in0=ch["n"][:], in1=ch["guess"][:], op=ALU.mult)

        def guess_times_g(ch):
            g_chunk = g_raw[:].rearrange("p c t o -> p (c t) o")[:, :, ch["k"] * CHUNK_OUT : (ch["k"] + 1) * CHUNK_OUT]
            ch["gg"] = four.tile([P, GROUPS], F32, name="gg")
            nc.gpsimd.tensor_tensor(out=by_slice(ch["gg"][:]), in0=by_slice(ch["guess"][:]), in1=g_chunk, op=ALU.mult)

        def scale_g(ch):
            ch["u"] = two.tile([P, GROUPS], F32, name="u")
            nc.vector.scalar_tensor_tensor(
                out=ch["u"][:], in0=ch["ng"][:], scalar=2.0, in1=ch["gg"][:], op0=ALU.subtract, op1=ALU.mult
            )

        def weigh(ch, passes=range(PASSES)):
            groups = slice(passes.start * GROUPS // PASSES, passes.stop * GROUPS // PASSES)
            w = flat(ch["w"][:, groups, :])
            nc.vector.tensor_tensor(out=w, in0=w, in1=flat(ch["is_top"][:, groups, :]), op=ALU.subtract)

        def times_g(ch, share):
            cut = GROUPS - share
            nc.vector.tensor_tensor(
                out=groups_of(ch["e"][:])[:, :cut, :],
                in0=groups_of(ch["e"][:])[:, :cut, :],
                in1=ch["u_ps"][:, :cut].unsqueeze(2).to_broadcast([P, cut, ND]),
                op=ALU.mult,
            )

        def times_g_rest(ch, share):
            cut = GROUPS - share
            nc.gpsimd.tensor_tensor(
                out=groups_of(ch["e"][:])[:, cut:, :],
                in0=groups_of(ch["e"][:])[:, cut:, :],
                in1=ch["u"][:, cut:].unsqueeze(2).to_broadcast([P, share, ND]),
                op=ALU.mult,
            )

        def times_w(ch, engine, passes):
            groups = slice(passes.start * GROUPS // PASSES, passes.stop * GROUPS // PASSES)
            e = groups_of(ch["e"][:])[:, groups, :]
            engine.tensor_tensor(out=e, in0=e, in1=ch["w"][:, groups, :], op=ALU.mult)

        def round_e(ch):
            start_round(ch)
            for c in range(PASSES):
                round_pass(ch, c)

        def start_round(ch):
            ch["e_grouped"] = two.tile([P, PASSES, CHUNK, PACK], BF16, align_bytes=64, name="e_grouped")

        def round_pass(ch, c):
            regroup(nc, ch["e_grouped"][:, c], ch["e"][:, c])

        def quantise_e(ch):
            ch["codes"] = two.tile([P, PASSES, CHUNK], U32, align_bytes=64, name="e_codes")
            ch["scales"] = two.tile([P, PASSES, CHUNK], U8, align_bytes=64, name="e_scales")
            nc.vector.quantize_mx(
                out=ch["codes"][:].rearrange("p c j -> p (c j)").bitcast(E5M2_X4),
                scales=ch["scales"][:].rearrange("p c j -> p (c j)"),
                in_=ch["e_grouped"][:].rearrange("p c j t -> p (c j t)"),
            )

        x_grouped = [keep.tile([P, IN, PACK], BF16, align_bytes=64, name="x_grouped%d" % c) for c in range(PASSES)]

        def regroup_x(c, h):
            n_cols = slice(h * N_TILE, (h + 1) * N_TILE)
            regroup(nc, x_grouped[c][:, n_cols, :], x_raw[c, h][:])

        def quantise_x(c):
            nc.vector.quantize_mx(
                out=x_codes[:, c].bitcast(E4M3_X4),
                scales=x_scales[:, c],
                in_=x_grouped[c][:].rearrange("p i t -> p (i t)"),
            )

        def turn(out, block, start, stop):
            nc.tensor.matmul(out=out, lhsT=block, rhs=identity[:], is_transpose=True, start=start, stop=stop)

        def sum_tokens(ch):
            ch["sums"] = acc_pool.tile([P, CHUNK_TILES, P], F32, name="acc")
            for a in range(CHUNK_TILES):
                for s in range(SLICES):
                    block = ch["e"][:, s // PACK, s % PACK, a * M_TILE : (a + 1) * M_TILE]
                    turn(ch["sums"][:, a, :], block, s == 0, s == SLICES - 1)

        def negate(ch):
            ch["neg_r"] = two.tile([P, CHUNK_TILES], F32, name="neg_r")
            for a in range(CHUNK_TILES):
                scrap = two.tile([P, P], F32, name="scrap")
                nc.scalar.activation(
                    out=scrap[:], in_=ch["sums"][:, a, :], func=ACT.Copy, scale=-1.0, accum_out=ch["neg_r"][:, a : a + 1]
                )

        def multiply(ch):
            ch["acc"] = []
            for a in range(CHUNK_TILES):
                rows = slice(a * M_TILE, (a + 1) * M_TILE)
                for h in range(IN // N_TILE):
                    n_cols = slice(h * N_TILE, (h + 1) * N_TILE)
                    acc = acc_pool.tile([P, N_TILE], F32, name="acc")
                    for c in range(PASSES):
                        nc.tensor.matmul_mx(
                            out=acc[:],
                            lhsT=ch["codes"][:, c, rows].bitcast(E5M2_X4),
                            lhsT_scale=ch["scales"][:, c, rows],
                            rhs=x_codes[:, c, n_cols].bitcast(E4M3_X4),
                            rhs_scale=x_scales[:, c, n_cols],
                            start=(c == 0),
                            stop=(c == PASSES - 1),
                        )
                    ch["acc"].append((a, n_cols, acc))

        def finish(ch, tiles=range(CHUNK_TILES)):
            results = {a: outs.tile([P, IN], F32, name="result") for a in tiles}
            for a, n_cols, acc in [block for block in ch["acc"] if block[0] in tiles]:
                first = ch["k"] * CHUNK + a * M_TILE
                parts = 2 if first + M_TILE == ROWS and n_cols.stop == IN else 1
                width = N_TILE // parts
                for n0 in range(0, N_TILE, width):
                    cols = slice(n_cols.start + n0, n_cols.start + n0 + width)
                    nc.vector.scalar_tensor_tensor(
                        out=results[a][:, cols],
                        in0=centers_sb[ch["k"]][:, a, cols],
                        scalar=ch["neg_r"][:, a : a + 1],
                        in1=acc[:, n0 : n0 + width],
                        op0=ALU.mult,
                        op1=ALU.add,
                    )
                    nc.sync.dma_start(out=out_rows[first : first + M_TILE, cols], in_=results[a][:, cols])

        chunks = [{"k": k, "e": probs_sb[k]} for k in range(CHUNKS)]
        LAST = CHUNKS - 1

        def at(k):
            return chunks[k : k + 1] if k >= 0 else []

        def gpsimd_share(k):
            if k == 0:
                return 3 * GROUPS // 4
            if 2 <= k <= 4:
                return GROUPS // 2
            return GROUPS // 4 if k in (1, 5) else 0

        for k in range(-3, CHUNKS + 2):
            done, ended, now, soon = at(k - 2), at(k - 1), at(k), at(k + 1)
            drain = k >= LAST - 1
            both(count_8_to_4, soon)
            both(nine_tops, soon)
            both(count_4_to_1, soon)
            if k != LAST:
                both(scale_g, now)
                both(u_to_psum, now)
            both(guess_inverse, soon)
            if k - 1 != LAST:
                both(negate, done)
            both(expand_n, soon)
            if k == -2:
                regroup_x(0, 0)
            if k == 0:
                regroup_x(0, 1)
            if k == 1:
                regroup_x(1, 0)
                regroup_x(1, 1)
            if k == 2:
                quantise_x(0)
            if k - 1 == LAST:
                for ch in ended:
                    weigh(ch, range(0, 1))
                    times_w(ch, nc.vector, range(0, 1))
                    both(quantise_e, done)
                    both(multiply, done)
                    weigh(ch, range(1, PASSES))
                    times_w(ch, nc.vector, range(1, PASSES))
                    start_round(ch)
                    round_pass(ch, 0)
                    both(negate, done)
                    round_pass(ch, 1)
                    sum_tokens(ch)
            elif k - 2 < LAST:
                if k != 2 and k != LAST:
                    both(quantise_e, done)
                    both(multiply, done)
                    both(weigh, ended)
                elif k == LAST:
                    for ch in ended:
                        weigh(ch, range(1, PASSES))
                        both(quantise_e, done)
                        both(scale_g, now)
                        both(u_to_psum, now)
                        both(multiply, done)
                        weigh(ch, range(0, 1))
                else:
                    both(weigh, ended)
                for ch in ended:
                    if drain:
                        times_w(ch, nc.gpsimd, range(0, 1))
                        times_w(ch, nc.gpsimd, range(1, PASSES))
                    else:
                        times_w(ch, nc.gpsimd, range(0, PASSES))
            for ch in now:
                if gpsimd_share(k):
                    times_g_rest(ch, gpsimd_share(k))
            both(guess_times_g, soon)
            if k == -2:
                both(mark_top, at(0))
                both(find_top, at(1))
            else:
                both(find_top, at(k + 3))
                both(mark_top, at(k + 2))
            if k > -3:
                both(top_to_psum, at(k + 3))
            if k == 2:
                quantise_x(1)
                both(quantise_e, done)
                both(multiply, done)
            if drain or k == 2:
                for ch in now:
                    times_g(ch, gpsimd_share(k))
            if k - 1 == LAST:
                for ch in done:
                    finish(ch, range(0, 1))
                both(quantise_e, ended)
                for ch in done:
                    finish(ch, range(1, CHUNK_TILES))
                both(multiply, ended)
            else:
                both(finish, done)
            both(newton_1, soon)
            if not (drain or k == 2):
                for ch in now:
                    times_g(ch, gpsimd_share(k))
            if k - 1 < LAST:
                both(round_e, ended)
                both(sum_tokens, ended)
